import numpy as np
import ml_dtypes


def mxq(x, axis, fmt="e4m3"):
    dtype, down = {"e4m3": (ml_dtypes.float8_e4m3fn, 7), "e5m2": (ml_dtypes.float8_e5m2, 14)}[fmt]
    v = np.moveaxis(np.asarray(x, np.float32).astype(ml_dtypes.bfloat16).astype(np.float64), axis, -1)
    blocks = v.reshape(v.shape[:-1] + (-1, 32))
    amax = np.abs(blocks).max(-1, keepdims=True)
    byte = np.maximum(np.where(amax > 0, np.frexp(amax)[1] - 1 + 127, 0) - down, 1)
    scale = np.exp2(byte - 127.0)
    codes = (blocks / scale).astype(np.float32).astype(dtype).astype(np.float64)
    return np.moveaxis((codes * scale).reshape(v.shape), -1, axis)


WIDE = False


def mx_kscale(k):
    if not WIDE:
        return np.ones(k)
    levels = np.array([10, -10, 5, -5, 0])
    a = np.random.permutation(np.resize(levels, k // 512 * 4)).reshape(k // 512, 4)
    idx = np.arange(k)
    return np.exp2(a[idx // 512, idx % 128 // 32])


BF16 = ml_dtypes.bfloat16


def bf(x):
    return np.asarray(x, np.float32).astype(BF16)


def f64(x):
    return np.asarray(x).astype(np.float64)


B, C, P, D = 16, 512, 128, 512
EPS = 1e-5
SIG = 1.9
GTOP = 2.0 ** -12
RE = 2.0 ** -8


def layer_norm(v, w, b):
    m = v.mean(-1, keepdims=True)
    var = ((v - m) ** 2).mean(-1, keepdims=True)
    return (v - m) * (1.0 / np.sqrt(var + EPS)) * w + b


def setup_inputs():
    s = mx_kscale(C)
    wide = s.max() > s.min()
    g = s * (GTOP / s.max()) if wide else np.ones(C)
    k = RE / g if wide else np.ones(C)
    l = SIG * np.random.standard_normal((B, P, C))
    e = np.exp(l - l.max(-1, keepdims=True))
    mask = e / e.sum(-1, keepdims=True) * np.exp(0.2 * np.random.standard_normal((B, P, 1)))
    return {"x": bf(np.random.standard_normal((B, C))),
            "mask": bf(mask * k[None, None, :]),
            "feature_emb_weight": bf(np.random.standard_normal((C, D)) * g[:, None]),
            "feature_emb_bias": bf(0.5 * np.random.standard_normal((C, D)) * g[:, None]),
            "ln_emb_w": bf(1.0 + 0.1 * np.random.standard_normal(D)),
            "ln_emb_b": bf(0.1 * np.random.standard_normal(D) / k.max()),
            "W_exp": bf(0.5 * np.random.standard_normal(P)),
            "b_exp": bf(0.2 * np.random.standard_normal(P) / k.max())}


def reference(x, mask, feature_emb_weight, feature_emb_bias, ln_emb_w, ln_emb_b, W_exp, b_exp):
    m = f64(mask)
    pre = np.maximum(f64(x)[:, :, None] * f64(feature_emb_weight)[None] + f64(feature_emb_bias)[None], 0.0)
    x_emb = layer_norm(pre, f64(ln_emb_w), f64(ln_emb_b))
    agg = mxq(m, 2, "e4m3") @ mxq(x_emb, 1, "e4m3")
    return agg * (1.0 + f64(W_exp))[None, :, None] + f64(b_exp)[None, :, None] * m.sum(-1, keepdims=True)

@@ -1,0 +1,232 @@
+from contextlib import ExitStack
+
+import concourse.mybir as mybir
+from concourse.masks import make_identity
+
+F32 = mybir.dt.float32
+BF16 = mybir.dt.bfloat16
+U32 = mybir.dt.uint32
+U8 = mybir.dt.uint8
+FP8X4 = mybir.dt.float8_e4m3fn_x4
+ALU = mybir.AluOpType
+ACT = mybir.ActivationFunctionType
+
+SAMPLES = 16
+COLUMNS = 512
+PROMPTS = 128
+FEATURES = 512
+EPS = 1e-5
+
+P = 128
+PACK = 4
+PAIRS = 2
+FEATURE_BLOCKS = FEATURES // P
+HALF = FEATURES // 2
+MASK_GROUP = 4
+LARGEST_F32 = 3.4028234663852886e38
+
+FLOPS = 2 * SAMPLES * PROMPTS * COLUMNS * FEATURES
+
+
+def tile_tromptcell_pb_kernel(
+    tc, x, mask, feature_emb_weight, feature_emb_bias, ln_emb_w, ln_emb_b, W_exp, b_exp, out
+):
+    nc = tc.nc
+    with ExitStack() as ctx:
+        const = ctx.enter_context(tc.tile_pool(name="const", bufs=1))
+        work = ctx.enter_context(tc.tile_pool(name="work", bufs=2))
+        small = ctx.enter_context(tc.tile_pool(name="small", bufs=3))
+        psum_const = ctx.enter_context(tc.psum_pool(name="psum_const", bufs=1))
+        psum = ctx.enter_context(tc.psum_pool(name="psum", bufs=1))
+        ctx.enter_context(tc.manual_schedule())
+
+        b_sb = const.tile([P, PACK, FEATURES], BF16, name="b_sb")
+        nc.sync.dma_start(out=b_sb[:], in_=feature_emb_bias.rearrange("(p t) d -> p t d", t=PACK))
+        w_sb = const.tile([P, PACK, FEATURES], BF16, name="w_sb")
+        nc.sync.dma_start(out=w_sb[:], in_=feature_emb_weight.rearrange("(p t) d -> p t d", t=PACK))
+        x_sb = const.tile([P, SAMPLES, PACK], BF16, name="x_sb")
+        with nc.allow_non_contiguous_dma(reason="x is small; 8-byte pieces put c on the partitions"):
+            nc.scalar.dma_start(out=x_sb[:], in_=x.rearrange("n (p t) -> p n t", t=PACK))
+        rows = const.tile([P, P], BF16, name="rows")
+        nc.vector.memset(rows[:], 0.0)
+        nc.scalar.dma_start(out=rows[0:4, :], in_=ln_emb_w.rearrange("(b d) -> b d", d=P))
+        nc.scalar.dma_start(out=rows[4:8, :], in_=ln_emb_b.rearrange("(b d) -> b d", d=P))
+        nc.scalar.dma_start(out=rows[8:9, :], in_=W_exp.rearrange("(o q) -> o q", o=1))
+        nc.scalar.dma_start(out=rows[9:10, :], in_=b_exp.rearrange("(o q) -> o q", o=1))
+        mask_sb = const.tile([P, SAMPLES, COLUMNS], BF16, name="mask_sb")
+        for g in range(SAMPLES // MASK_GROUP):
+            group = slice(g * MASK_GROUP, (g + 1) * MASK_GROUP)
+            nc.sync.dma_start(out=mask_sb[:, group, :], in_=mask[group].rearrange("n q c -> q n c"))
+
+        ident_bf = const.tile([P, P], BF16, name="ident_bf")
+        make_identity(nc, ident_bf[:])
+        ident_f32 = const.tile([P, P], F32, name="ident_f32")
+        make_identity(nc, ident_f32[:])
+
+        bias_ps = [psum_const.tile([P, 2, FEATURES], BF16, name="bias_ps%d" % h) for h in range(2)]
+        for t in range(PACK):
+            nc.tensor.matmul(
+                out=bias_ps[t // 2][:, t % 2, :], lhsT=ident_bf[:], rhs=b_sb[:, t, :], start=True, stop=True
+            )
+
+        cols_ps = psum.tile([P, P], BF16, name="cols_ps", tag="acc")
+        nc.tensor.transpose(cols_ps[:], rows[:], ident_bf[:])
+        cols = const.tile([P, 16], F32, name="cols")
+        nc.scalar.copy(out=cols[:], in_=cols_ps[:, 0:16])
+        ln_w_col = [cols[:, b : b + 1] for b in range(FEATURE_BLOCKS)]
+        ln_b_col = [cols[:, FEATURE_BLOCKS + b : FEATURE_BLOCKS + b + 1] for b in range(FEATURE_BLOCKS)]
+        b_exp_col = cols[:, 9:10]
+        one_plus_w_exp = const.tile([P, 1], F32, name="one_plus_w_exp")
+        nc.gpsimd.tensor_scalar_add(out=one_plus_w_exp[:], in0=cols[:, 8:9], scalar1=1.0)
+
+        mask_words = const.tile([P, SAMPLES, PROMPTS, PAIRS], F32, name="mask_words", align_bytes=64)
+        mask_codes = const.tile([P, SAMPLES * PROMPTS], U32, name="mask_codes", align_bytes=64)
+        mask_scales = const.tile([P, SAMPLES * PROMPTS], U8, name="mask_scales", align_bytes=64)
+        out_bias = const.tile([P, SAMPLES], F32, name="out_bias")
+
+        act, moments, std, e_t, grouped = {}, {}, {}, {}, {}
+
+        def embed(n):
+            act[n] = work.tile([P, PACK, FEATURES], F32, name="act", bufs=5)
+            for t in range(PACK):
+                nc.vector.scalar_tensor_tensor(
+                    out=act[n][:, t, :],
+                    in0=w_sb[:, t, :],
+                    scalar=x_sb[:, n, t : t + 1],
+                    in1=bias_ps[t // 2][:, t % 2, :],
+                    op0=ALU.mult,
+                    op1=ALU.add,
+                )
+            nc.gpsimd.tensor_scalar(
+                out=act[n][:], in0=act[n][:], scalar1=LARGEST_F32, scalar2=0.0, op0=ALU.min, op1=ALU.max
+            )
+
+        def measure(n):
+            stats = small.tile([P, PACK, 6], F32, name="stats")
+            moments[n] = small.tile([P, PACK, 2], F32, name="moments")
+            for t in range(PACK):
+                nc.vector.bn_stats(out=stats[:, t, :], in_=act[n][:, t, :])
+            for t in range(PACK):
+                nc.vector.bn_aggr(out=moments[n][:, t, :], in_=stats[:, t, :])
+
+        def deviation(n):
+            var_eps = small.tile([P, PACK], F32, name="var_eps")
+            nc.vector.tensor_scalar_add(out=var_eps[:], in0=moments[n][:, :, 1], scalar1=EPS)
+            std[n] = small.tile([P, PACK], F32, name="std")
+            nc.scalar.activation(out=std[n][:], in_=var_eps[:], func=ACT.Sqrt)
+
+        def normalise(n):
+            rstd = small.tile([P, PACK], F32, name="rstd")
+            nc.vector.reciprocal(out=rstd[:], in_=std[n][:])
+            neg_mean = small.tile([P, PACK], F32, name="neg_mean")
+            nc.vector.tensor_scalar_mul(out=neg_mean[:], in0=moments[n][:, :, 0], scalar1=-1.0)
+            for t in range(PACK):
+                nc.gpsimd.tensor_scalar(
+                    out=act[n][:, t, :],
+                    in0=act[n][:, t, :],
+                    scalar1=neg_mean[:, t : t + 1],
+                    scalar2=rstd[:, t : t + 1],
+                    op0=ALU.add,
+                    op1=ALU.mult,
+                )
+
+        def to_features(n):
+            e_t[n] = work.tile([P, FEATURE_BLOCKS, COLUMNS], BF16, name="e_t")
+            for b in range(FEATURE_BLOCKS):
+                z_t = psum.tile([P, PACK, P], F32, name="z_t", tag="z_t", bufs=3)
+                for t in range(PACK):
+                    nc.tensor.transpose(z_t[:, t, :], act[n][:, t, b * P : (b + 1) * P], ident_f32[:])
+                nc.scalar.activation(
+                    out=e_t[n][:, b, :].rearrange("d (u p e) -> d u p e", u=PAIRS, e=2),
+                    in_=z_t[:].rearrange("d (u e) p -> d u p e", e=2),
+                    func=ACT.Identity,
+                    scale=ln_w_col[b],
+                    bias=ln_b_col[b],
+                )
+
+        def to_columns(n):
+            grouped[n] = work.tile([P, FEATURES, PAIRS], F32, name="grouped", align_bytes=64)
+            for h in range(FEATURES // HALF):
+                e_w = psum.tile([P, PAIRS, HALF], F32, name="e_w", tag="e_w", bufs=2)
+                for i in range(HALF // P):
+                    words = e_t[n][:, h * (HALF // P) + i, :].bitcast(F32)
+                    for u in range(PAIRS):
+                        nc.tensor.transpose(
+                            e_w[:, u, i * P : (i + 1) * P], words[:, u * P : (u + 1) * P], ident_f32[:]
+                        )
+                nc.scalar.copy(
+                    out=grouped[n][:, h * HALF : (h + 1) * HALF, :], in_=e_w[:].rearrange("p u d -> p d u")
+                )
+
+        def pool(n):
+            codes = work.tile([P, FEATURES], U32, name="codes", align_bytes=64)
+            scales = work.tile([P, FEATURES], U8, name="scales", align_bytes=64)
+            nc.vector.quantize_mx(
+                out=codes[:].bitcast(FP8X4),
+                scales=scales[:],
+                in_=grouped[n][:].rearrange("p d u -> p (d u)").bitcast(BF16),
+            )
+            prompts = slice(n * PROMPTS, (n + 1) * PROMPTS)
+            acc = psum.tile([P, FEATURES], F32, name="acc", tag="acc")
+            nc.tensor.matmul_mx(
+                out=acc[:],
+                lhsT=mask_codes[:, prompts].bitcast(FP8X4),
+                lhsT_scale=mask_scales[:, prompts],
+                rhs=codes[:].bitcast(FP8X4),
+                rhs_scale=scales[:],
+                start=True,
+                stop=True,
+            )
+            result = work.tile([P, FEATURES], F32, name="result", bufs=3)
+            nc.scalar.activation(
+                out=result[:],
+                in_=acc[:],
+                func=ACT.Identity,
+                scale=one_plus_w_exp[:, 0:1],
+                bias=out_bias[:, n : n + 1],
+            )
+            nc.sync.dma_start(out=out[n], in_=result[:])
+
+        def row_sum(n):
+            scaled = work.tile([P, COLUMNS], BF16, name="scaled", bufs=3)
+            nc.scalar.activation(
+                out=scaled[:], in_=mask_sb[:, n, :], func=ACT.Copy, scale=b_exp_col, accum_out=out_bias[:, n : n + 1]
+            )
+
+        def transpose_mask(g):
+            for first in range(g * MASK_GROUP, (g + 1) * MASK_GROUP, 2):
+                m_t = psum.tile([P, 2, PAIRS, PROMPTS], F32, name="m_t", tag="z_t", bufs=3)
+                for s in range(2):
+                    words = mask_sb[:, first + s, :].bitcast(F32).rearrange("q (p u) -> q u p", u=PAIRS)
+                    for u in range(PAIRS):
+                        nc.tensor.transpose(m_t[:, s, u, :], words[:, u, :], ident_f32[:])
+                nc.scalar.copy(
+                    out=mask_words[:, first : first + 2, :, :], in_=m_t[:].rearrange("p s u q -> p s q u")
+                )
+
+        def quantise_mask(g):
+            prompts = slice(g * MASK_GROUP * PROMPTS, (g + 1) * MASK_GROUP * PROMPTS)
+            nc.vector.quantize_mx(
+                out=mask_codes[:, prompts].bitcast(FP8X4),
+                scales=mask_scales[:, prompts],
+                in_=mask_words[:, g * MASK_GROUP : (g + 1) * MASK_GROUP, :, :]
+                .rearrange("p n q u -> p (n q u)")
+                .bitcast(BF16),
+            )
+
+        def due(stage, index, count):
+            if 0 <= index < count:
+                stage(index)
+
+        mask_groups = SAMPLES // MASK_GROUP
+        for j in range(SAMPLES + 4):
+            due(embed, j, SAMPLES)
+            due(quantise_mask, j - 2, mask_groups)
+            due(normalise, j - 2, SAMPLES)
+            due(to_features, j - 3, SAMPLES)
+            due(measure, j - 1, SAMPLES)
+            due(pool, j - 4, SAMPLES)
+            due(deviation, j - 1, SAMPLES)
+            due(to_columns, j - 3, SAMPLES)
+            due(row_sum, j, SAMPLES)
+            due(transpose_mask, j, mask_groups)

@@ -84,7 +84,7 @@ def tile_tromptcell_pb_kernel(
         mask_scales = const.tile([P, SAMPLES * PROMPTS], U8, name="mask_scales", align_bytes=64)
         out_bias = const.tile([P, SAMPLES], F32, name="out_bias")
 
-        act, moments, std, e_t, grouped = {}, {}, {}, {}, {}
+        act, moments, std, neg_mean, e_t, grouped = {}, {}, {}, {}, {}, {}
 
         def embed(n):
             act[n] = work.tile([P, PACK, FEATURES], F32, name="act", bufs=5)
@@ -110,21 +110,19 @@ def tile_tromptcell_pb_kernel(
                 nc.vector.bn_aggr(out=moments[n][:, t, :], in_=stats[:, t, :])
 
         def deviation(n):
-            var_eps = small.tile([P, PACK], F32, name="var_eps")
-            nc.vector.tensor_scalar_add(out=var_eps[:], in0=moments[n][:, :, 1], scalar1=EPS)
             std[n] = small.tile([P, PACK], F32, name="std")
-            nc.scalar.activation(out=std[n][:], in_=var_eps[:], func=ACT.Sqrt)
+            nc.scalar.activation(out=std[n][:], in_=moments[n][:, :, 1], func=ACT.Sqrt, bias=EPS)
+            neg_mean[n] = small.tile([P, PACK], F32, name="neg_mean")
+            nc.scalar.activation(out=neg_mean[n][:], in_=moments[n][:, :, 0], func=ACT.Copy, scale=-1.0)
 
         def normalise(n):
             rstd = small.tile([P, PACK], F32, name="rstd")
             nc.vector.reciprocal(out=rstd[:], in_=std[n][:])
-            neg_mean = small.tile([P, PACK], F32, name="neg_mean")
-            nc.vector.tensor_scalar_mul(out=neg_mean[:], in0=moments[n][:, :, 0], scalar1=-1.0)
             for t in range(PACK):
                 nc.gpsimd.tensor_scalar(
                     out=act[n][:, t, :],
                     in0=act[n][:, t, :],
-                    scalar1=neg_mean[:, t : t + 1],
+                    scalar1=neg_mean[n][:, t : t + 1],
                     scalar2=rstd[:, t : t + 1],
                     op0=ALU.add,
                     op1=ALU.mult,

@@ -83,6 +83,9 @@ def tile_tromptcell_pb_kernel(
         mask_codes = const.tile([P, SAMPLES * PROMPTS], U32, name="mask_codes", align_bytes=64)
         mask_scales = const.tile([P, SAMPLES * PROMPTS], U8, name="mask_scales", align_bytes=64)
         out_bias = const.tile([P, SAMPLES], F32, name="out_bias")
+        ones = const.tile([P, 16], BF16, name="ones")
+        nc.vector.memset(ones[:], 1.0)
+        sums = psum.tile([P, SAMPLES], F32, name="sums", tag="acc")
 
         act, moments, std, neg_mean, e_t, grouped = {}, {}, {}, {}, {}, {}
 
@@ -97,9 +100,11 @@ def tile_tromptcell_pb_kernel(
                     op0=ALU.mult,
                     op1=ALU.add,
                 )
-            nc.gpsimd.tensor_scalar(
-                out=act[n][:], in0=act[n][:], scalar1=LARGEST_F32, scalar2=0.0, op0=ALU.min, op1=ALU.max
-            )
+            mine = act[n][:, 0 : PACK - 1, :]
+            nc.gpsimd.tensor_scalar(out=mine, in0=mine, scalar1=LARGEST_F32, scalar2=0.0, op0=ALU.min, op1=ALU.max)
+
+        def relu_last(n):
+            nc.scalar.activation(out=act[n][:, PACK - 1, :], in_=act[n][:, PACK - 1, :], func=ACT.Relu)
 
         def measure(n):
             stats = small.tile([P, PACK, 6], F32, name="stats")
@@ -185,11 +190,19 @@ def tile_tromptcell_pb_kernel(
             )
             nc.sync.dma_start(out=out[n], in_=result[:])
 
-        def row_sum(n):
-            scaled = work.tile([P, COLUMNS], BF16, name="scaled", bufs=3)
-            nc.scalar.activation(
-                out=scaled[:], in_=mask_sb[:, n, :], func=ACT.Copy, scale=b_exp_col, accum_out=out_bias[:, n : n + 1]
-            )
+        def row_sums(g):
+            for n in range(g * MASK_GROUP, (g + 1) * MASK_GROUP):
+                values = (
+                    mask_words[:, n, :, :].rearrange("p q u -> p (q u)").bitcast(BF16)
+                    .rearrange("p (q t) -> p t q", t=PACK)
+                )
+                for t in range(PACK):
+                    nc.tensor.matmul(
+                        out=sums[:, n : n + 1], lhsT=values[:, t, :], rhs=ones[:, 0:1],
+                        start=(t == 0), stop=(t == PACK - 1),
+                    )
+            if g == SAMPLES // MASK_GROUP - 1:
+                nc.scalar.activation(out=out_bias[:], in_=sums[:], func=ACT.Copy, scale=b_exp_col)
 
         def transpose_mask(g):
             for first in range(g * MASK_GROUP, (g + 1) * MASK_GROUP, 2):
@@ -226,5 +239,6 @@ def tile_tromptcell_pb_kernel(
             due(pool, j - 4, SAMPLES)
             due(deviation, j - 1, SAMPLES)
             due(to_columns, j - 3, SAMPLES)
-            due(row_sum, j, SAMPLES)
+            due(relu_last, j, SAMPLES)
             due(transpose_mask, j, mask_groups)
+            due(row_sums, j, mask_groups)

@@ -24,6 +24,7 @@ FEATURE_BLOCKS = FEATURES // P
 HALF = FEATURES // 2
 MASK_GROUP = 4
 LARGEST_F32 = 3.4028234663852886e38
+LAST = PACK - 1
 
 FLOPS = 2 * SAMPLES * PROMPTS * COLUMNS * FEATURES
 
@@ -87,7 +88,7 @@ def tile_tromptcell_pb_kernel(
         nc.vector.memset(ones[:], 1.0)
         sums = psum.tile([P, SAMPLES], F32, name="sums", tag="acc")
 
-        act, moments, std, neg_mean, e_t, grouped = {}, {}, {}, {}, {}, {}
+        act, moments, std, neg_mean, e_t, grouped, total, spread = {}, {}, {}, {}, {}, {}, {}, {}
 
         def embed(n):
             act[n] = work.tile([P, PACK, FEATURES], F32, name="act", bufs=5)
@@ -100,25 +101,44 @@ def tile_tromptcell_pb_kernel(
                     op0=ALU.mult,
                     op1=ALU.add,
                 )
-            mine = act[n][:, 0 : PACK - 1, :]
+            mine = act[n][:, 0:LAST, :]
             nc.gpsimd.tensor_scalar(out=mine, in0=mine, scalar1=LARGEST_F32, scalar2=0.0, op0=ALU.min, op1=ALU.max)
 
         def relu_last(n):
-            nc.scalar.activation(out=act[n][:, PACK - 1, :], in_=act[n][:, PACK - 1, :], func=ACT.Relu)
+            total[n] = small.tile([P, 1], F32, name="total")
+            nc.scalar.activation(
+                out=act[n][:, LAST, :], in_=act[n][:, LAST, :], func=ACT.Relu, accum_out=total[n][:]
+            )
+
+        def centre_last(n):
+            neg_mean[n] = small.tile([P, PACK], F32, name="neg_mean")
+            nc.scalar.activation(
+                out=neg_mean[n][:, LAST : LAST + 1], in_=total[n][:], func=ACT.Copy, scale=-1.0 / FEATURES
+            )
+
+        def square_last(n):
+            squares = work.tile([P, FEATURES], BF16, name="squares")
+            spread[n] = small.tile([P, 1], F32, name="spread")
+            nc.scalar.activation(
+                out=squares[:], in_=act[n][:, LAST, :], func=ACT.Square,
+                bias=neg_mean[n][:, LAST : LAST + 1], accum_out=spread[n][:],
+            )
 
         def measure(n):
-            stats = small.tile([P, PACK, 6], F32, name="stats")
-            moments[n] = small.tile([P, PACK, 2], F32, name="moments")
-            for t in range(PACK):
+            stats = small.tile([P, LAST, 6], F32, name="stats")
+            moments[n] = small.tile([P, LAST, 2], F32, name="moments")
+            for t in range(LAST):
                 nc.vector.bn_stats(out=stats[:, t, :], in_=act[n][:, t, :])
-            for t in range(PACK):
+            for t in range(LAST):
                 nc.vector.bn_aggr(out=moments[n][:, t, :], in_=stats[:, t, :])
 
         def deviation(n):
             std[n] = small.tile([P, PACK], F32, name="std")
-            nc.scalar.activation(out=std[n][:], in_=moments[n][:, :, 1], func=ACT.Sqrt, bias=EPS)
-            neg_mean[n] = small.tile([P, PACK], F32, name="neg_mean")
-            nc.scalar.activation(out=neg_mean[n][:], in_=moments[n][:, :, 0], func=ACT.Copy, scale=-1.0)
+            nc.scalar.activation(out=std[n][:, 0:LAST], in_=moments[n][:, :, 1], func=ACT.Sqrt, bias=EPS)
+            nc.scalar.activation(
+                out=std[n][:, LAST : LAST + 1], in_=spread[n][:], func=ACT.Sqrt, scale=1.0 / FEATURES, bias=EPS
+            )
+            nc.scalar.activation(out=neg_mean[n][:, 0:LAST], in_=moments[n][:, :, 0], func=ACT.Copy, scale=-1.0)
 
         def normalise(n):
             rstd = small.tile([P, PACK], F32, name="rstd")
@@ -234,7 +254,9 @@ def tile_tromptcell_pb_kernel(
             due(embed, j, SAMPLES)
             due(quantise_mask, j - 2, mask_groups)
             due(normalise, j - 2, SAMPLES)
+            due(centre_last, j - 1, SAMPLES)
             due(to_features, j - 3, SAMPLES)
+            due(square_last, j - 1, SAMPLES)
             due(measure, j - 1, SAMPLES)
             due(pool, j - 4, SAMPLES)
             due(deviation, j - 1, SAMPLES)

@@ -257,10 +257,10 @@ def tile_tromptcell_pb_kernel(
             due(centre_last, j - 1, SAMPLES)
             due(to_features, j - 3, SAMPLES)
             due(square_last, j - 1, SAMPLES)
-            due(measure, j - 1, SAMPLES)
-            due(pool, j - 4, SAMPLES)
-            due(deviation, j - 1, SAMPLES)
             due(to_columns, j - 3, SAMPLES)
             due(relu_last, j, SAMPLES)
+            due(measure, j - 1, SAMPLES)
+            due(deviation, j - 1, SAMPLES)
+            due(pool, j - 4, SAMPLES)
             due(transpose_mask, j, mask_groups)
             due(row_sums, j, mask_groups)

@@ -41,13 +41,18 @@ def tile_tromptcell_pb_kernel(
         psum = ctx.enter_context(tc.psum_pool(name="psum", bufs=1))
         ctx.enter_context(tc.manual_schedule())
 
-        b_sb = const.tile([P, PACK, FEATURES], BF16, name="b_sb")
-        nc.sync.dma_start(out=b_sb[:], in_=feature_emb_bias.rearrange("(p t) d -> p t d", t=PACK))
-        w_sb = const.tile([P, PACK, FEATURES], BF16, name="w_sb")
-        nc.sync.dma_start(out=w_sb[:], in_=feature_emb_weight.rearrange("(p t) d -> p t d", t=PACK))
-        x_sb = const.tile([P, SAMPLES, PACK], BF16, name="x_sb")
-        with nc.allow_non_contiguous_dma(reason="x is small; 8-byte pieces put c on the partitions"):
-            nc.scalar.dma_start(out=x_sb[:], in_=x.rearrange("n (p t) -> p n t", t=PACK))
+        x_rows = const.tile([P, COLUMNS], BF16, name="x_rows")
+        nc.scalar.dma_start(out=x_rows[0:SAMPLES, :], in_=x)
+        nc.scalar.dma_start(out=x_rows[SAMPLES : 2 * SAMPLES, :], in_=x)
+        nc.vector.memset(x_rows[32:64, :], 0.0)
+        nc.vector.memset(x_rows[64:128, :], 0.0)
+        b_view = feature_emb_bias.rearrange("(p t) d -> p t d", t=PACK)
+        w_view = feature_emb_weight.rearrange("(p t) d -> p t d", t=PACK)
+        b_sb = [const.tile([P, FEATURES], BF16, name="b_sb%d" % t) for t in range(PACK)]
+        w_sb = [const.tile([P, FEATURES], BF16, name="w_sb%d" % t) for t in range(PACK)]
+        for t in range(PACK):
+            nc.sync.dma_start(out=b_sb[t][:], in_=b_view[:, t, :])
+            nc.sync.dma_start(out=w_sb[t][:], in_=w_view[:, t, :])
         rows = const.tile([P, P], BF16, name="rows")
         nc.vector.memset(rows[:], 0.0)
         nc.scalar.dma_start(out=rows[0:4, :], in_=ln_emb_w.rearrange("(b d) -> b d", d=P))
@@ -64,10 +69,16 @@ def tile_tromptcell_pb_kernel(
         ident_f32 = const.tile([P, P], F32, name="ident_f32")
         make_identity(nc, ident_f32[:])
 
+        x_ps = psum.tile([P, PACK, P], BF16, name="x_ps", tag="e_w", bufs=2)
+        for t in range(PACK):
+            nc.tensor.transpose(x_ps[:, t, :], x_rows[:].rearrange("n (p t) -> n t p", t=PACK)[:, t, :], ident_bf[:])
+        x_sb = const.tile([P, SAMPLES, PACK], BF16, name="x_sb")
+        nc.scalar.copy(out=x_sb[:], in_=x_ps[:, :, 0:SAMPLES].rearrange("p t n -> p n t"))
+
         bias_ps = [psum_const.tile([P, 2, FEATURES], BF16, name="bias_ps%d" % h) for h in range(2)]
         for t in range(PACK):
             nc.tensor.matmul(
-                out=bias_ps[t // 2][:, t % 2, :], lhsT=ident_bf[:], rhs=b_sb[:, t, :], start=True, stop=True
+                out=bias_ps[t // 2][:, t % 2, :], lhsT=ident_bf[:], rhs=b_sb[t][:], start=True, stop=True
             )
 
         cols_ps = psum.tile([P, P], BF16, name="cols_ps", tag="acc")
@@ -95,7 +106,7 @@ def tile_tromptcell_pb_kernel(
             for t in range(PACK):
                 nc.vector.scalar_tensor_tensor(
                     out=act[n][:, t, :],
-                    in0=w_sb[:, t, :],
+                    in0=w_sb[t][:],
                     scalar=x_sb[:, n, t : t + 1],
                     in1=bias_ps[t // 2][:, t % 2, :],
                     op0=ALU.mult,

@@ -44,6 +44,9 @@ def tile_tromptcell_pb_kernel(
         x_rows = const.tile([P, COLUMNS], BF16, name="x_rows")
         nc.scalar.dma_start(out=x_rows[0:SAMPLES, :], in_=x)
         nc.scalar.dma_start(out=x_rows[SAMPLES : 2 * SAMPLES, :], in_=x)
+        warm = const.tile([P, 1], F32, name="warm")
+        nc.gpsimd.memset(warm[:], 1.0)
+        nc.scalar.activation(out=warm[:], in_=warm[:], func=ACT.Sqrt)
         nc.vector.memset(x_rows[32:64, :], 0.0)
         nc.vector.memset(x_rows[64:128, :], 0.0)
         b_view = feature_emb_bias.rearrange("(p t) d -> p t d", t=PACK)
@@ -73,7 +76,7 @@ def tile_tromptcell_pb_kernel(
         for t in range(PACK):
             nc.tensor.transpose(x_ps[:, t, :], x_rows[:].rearrange("n (p t) -> n t p", t=PACK)[:, t, :], ident_bf[:])
         x_sb = const.tile([P, SAMPLES, PACK], BF16, name="x_sb")
-        nc.scalar.copy(out=x_sb[:], in_=x_ps[:, :, 0:SAMPLES].rearrange("p t n -> p n t"))
+        nc.vector.tensor_copy(out=x_sb[:], in_=x_ps[:, :, 0:SAMPLES].rearrange("p t n -> p n t"))
 
         bias_ps = [psum_const.tile([P, 2, FEATURES], BF16, name="bias_ps%d" % h) for h in range(2)]
         for t in range(PACK):

@@ -103,6 +103,7 @@ def tile_tromptcell_pb_kernel(
         sums = psum.tile([P, SAMPLES], F32, name="sums", tag="acc")
 
         act, moments, std, neg_mean, e_t, grouped, total, spread = {}, {}, {}, {}, {}, {}, {}, {}
+        rstd, z_t, e_w, codes, scales, acc = {}, {}, {}, {}, {}, {}
 
         def embed(n):
             act[n] = work.tile([P, PACK, FEATURES], F32, name="act", bufs=5)
@@ -154,75 +155,105 @@ def tile_tromptcell_pb_kernel(
             )
             nc.scalar.activation(out=neg_mean[n][:, 0:LAST], in_=moments[n][:, :, 0], func=ACT.Copy, scale=-1.0)
 
-        def normalise(n):
-            rstd = small.tile([P, PACK], F32, name="rstd")
-            nc.vector.reciprocal(out=rstd[:], in_=std[n][:])
+        def invert(n):
+            rstd[n] = small.tile([P, PACK], F32, name="rstd")
+            nc.vector.reciprocal(out=rstd[n][:], in_=std[n][:])
+
+        def normalise(n, on_vector=False):
+            engine = nc.vector if on_vector else nc.gpsimd
             for t in range(PACK):
-                nc.gpsimd.tensor_scalar(
+                engine.tensor_scalar(
                     out=act[n][:, t, :],
                     in0=act[n][:, t, :],
                     scalar1=neg_mean[n][:, t : t + 1],
-                    scalar2=rstd[:, t : t + 1],
+                    scalar2=rstd[n][:, t : t + 1],
                     op0=ALU.add,
                     op1=ALU.mult,
                 )
 
-        def to_features(n):
-            e_t[n] = work.tile([P, FEATURE_BLOCKS, COLUMNS], BF16, name="e_t")
-            for b in range(FEATURE_BLOCKS):
-                z_t = psum.tile([P, PACK, P], F32, name="z_t", tag="z_t", bufs=3)
-                for t in range(PACK):
-                    nc.tensor.transpose(z_t[:, t, :], act[n][:, t, b * P : (b + 1) * P], ident_f32[:])
-                nc.scalar.activation(
-                    out=e_t[n][:, b, :].rearrange("d (u p e) -> d u p e", u=PAIRS, e=2),
-                    in_=z_t[:].rearrange("d (u e) p -> d u p e", e=2),
-                    func=ACT.Identity,
-                    scale=ln_w_col[b],
-                    bias=ln_b_col[b],
-                )
+        def turn_to_features(n, b):
+            z_t[n, b] = psum.tile([P, PACK, P], F32, name="z_t", tag="z_t", bufs=3)
+            for t in range(PACK):
+                nc.tensor.transpose(z_t[n, b][:, t, :], act[n][:, t, b * P : (b + 1) * P], ident_f32[:])
 
-        def to_columns(n):
-            grouped[n] = work.tile([P, FEATURES, PAIRS], F32, name="grouped", align_bytes=64)
-            for h in range(FEATURES // HALF):
-                e_w = psum.tile([P, PAIRS, HALF], F32, name="e_w", tag="e_w", bufs=2)
-                for i in range(HALF // P):
-                    words = e_t[n][:, h * (HALF // P) + i, :].bitcast(F32)
-                    for u in range(PAIRS):
-                        nc.tensor.transpose(
-                            e_w[:, u, i * P : (i + 1) * P], words[:, u * P : (u + 1) * P], ident_f32[:]
-                        )
-                nc.scalar.copy(
-                    out=grouped[n][:, h * HALF : (h + 1) * HALF, :], in_=e_w[:].rearrange("p u d -> p d u")
+        def affine(n, b, on_vector=False):
+            if b == 0:
+                e_t[n] = work.tile([P, FEATURE_BLOCKS, COLUMNS], BF16, name="e_t")
+            target = e_t[n][:, b, :].rearrange("d (u p e) -> d u p e", u=PAIRS, e=2)
+            source = z_t[n, b][:].rearrange("d (u e) p -> d u p e", e=2)
+            if on_vector:
+                nc.vector.tensor_scalar(
+                    out=target, in0=source, scalar1=ln_w_col[b], scalar2=ln_b_col[b], op0=ALU.mult, op1=ALU.add
                 )
+            else:
+                nc.scalar.activation(out=target, in_=source, func=ACT.Identity, scale=ln_w_col[b], bias=ln_b_col[b])
 
-        def pool(n):
-            codes = work.tile([P, FEATURES], U32, name="codes", align_bytes=64)
-            scales = work.tile([P, FEATURES], U8, name="scales", align_bytes=64)
+        def turn_to_columns(n, h):
+            e_w[n, h] = psum.tile([P, PAIRS, HALF], F32, name="e_w", tag="e_w", bufs=2)
+            for i in range(HALF // P):
+                words = e_t[n][:, h * (HALF // P) + i, :].bitcast(F32)
+                for u in range(PAIRS):
+                    nc.tensor.transpose(
+                        e_w[n, h][:, u, i * P : (i + 1) * P], words[:, u * P : (u + 1) * P], ident_f32[:]
+                    )
+
+        def regroup(n, h, on_vector=False):
+            if h == 0:
+                grouped[n] = work.tile([P, FEATURES, PAIRS], F32, name="grouped", align_bytes=64)
+            target = grouped[n][:, h * HALF : (h + 1) * HALF, :]
+            source = e_w[n, h][:].rearrange("p u d -> p d u")
+            if on_vector:
+                nc.vector.tensor_copy(out=target, in_=source)
+            else:
+                nc.scalar.copy(out=target, in_=source)
+
+        def quantise(n):
+            codes[n] = work.tile([P, FEATURES], U32, name="codes", align_bytes=64)
+            scales[n] = work.tile([P, FEATURES], U8, name="scales", align_bytes=64)
             nc.vector.quantize_mx(
-                out=codes[:].bitcast(FP8X4),
-                scales=scales[:],
+                out=codes[n][:].bitcast(FP8X4),
+                scales=scales[n][:],
                 in_=grouped[n][:].rearrange("p d u -> p (d u)").bitcast(BF16),
             )
+
+        def multiply(n):
             prompts = slice(n * PROMPTS, (n + 1) * PROMPTS)
-            acc = psum.tile([P, FEATURES], F32, name="acc", tag="acc")
+            acc[n] = psum.tile([P, FEATURES], F32, name="acc", tag="acc")
             nc.tensor.matmul_mx(
-                out=acc[:],
+                out=acc[n][:],
                 lhsT=mask_codes[:, prompts].bitcast(FP8X4),
                 lhsT_scale=mask_scales[:, prompts],
-                rhs=codes[:].bitcast(FP8X4),
-                rhs_scale=scales[:],
+                rhs=codes[n][:].bitcast(FP8X4),
+                rhs_scale=scales[n][:],
                 start=True,
                 stop=True,
             )
+
+        def finish(n):
             result = work.tile([P, FEATURES], F32, name="result", bufs=3)
             nc.scalar.activation(
                 out=result[:],
-                in_=acc[:],
+                in_=acc[n][:],
                 func=ACT.Identity,
                 scale=one_plus_w_exp[:, 0:1],
                 bias=out_bias[:, n : n + 1],
             )
             nc.sync.dma_start(out=out[n], in_=result[:])
+
+        def to_features(n):
+            for b in range(FEATURE_BLOCKS):
+                turn_to_features(n, b)
+                affine(n, b)
+
+        def to_columns(n):
+            for h in range(FEATURES // HALF):
+                turn_to_columns(n, h)
+                regroup(n, h)
+
+        def pool(n):
+            quantise(n)
+            multiply(n)
+            finish(n)
 
         def row_sums(g):
             for n in range(g * MASK_GROUP, (g + 1) * MASK_GROUP):
@@ -264,9 +295,10 @@ def tile_tromptcell_pb_kernel(
                 stage(index)
 
         mask_groups = SAMPLES // MASK_GROUP
-        for j in range(SAMPLES + 4):
+        for j in range(SAMPLES):
             due(embed, j, SAMPLES)
             due(quantise_mask, j - 2, mask_groups)
+            due(invert, j - 2, SAMPLES)
             due(normalise, j - 2, SAMPLES)
             due(centre_last, j - 1, SAMPLES)
             due(to_features, j - 3, SAMPLES)
@@ -278,3 +310,41 @@ def tile_tromptcell_pb_kernel(
             due(pool, j - 4, SAMPLES)
             due(transpose_mask, j, mask_groups)
             due(row_sums, j, mask_groups)
+
+        a, b_, c, d = SAMPLES - 4, SAMPLES - 3, SAMPLES - 2, SAMPLES - 1
+        invert(c)
+        normalise(c)
+        measure(d)
+        centre_last(d)
+        square_last(d)
+        for b in range(2):
+            turn_to_features(b_, b)
+            affine(b_, b)
+        turn_to_features(b_, 2)
+        deviation(d)
+        quantise(a)
+        affine(b_, 2, on_vector=True)
+        turn_to_features(b_, 3)
+        affine(b_, 3, on_vector=True)
+        turn_to_columns(b_, 0)
+        regroup(b_, 0)
+        multiply(a)
+        finish(a)
+        invert(d)
+        normalise(d, on_vector=True)
+        turn_to_columns(b_, 1)
+        regroup(b_, 1)
+        quantise(b_)
+        for n in (c, d):
+            for b in range(FEATURE_BLOCKS):
+                turn_to_features(n, b)
+                affine(n, b, on_vector=(b % 2 == 1))
+            multiply(n - 1)
+            turn_to_columns(n, 0)
+            regroup(n, 0)
+            finish(n - 1)
+            turn_to_columns(n, 1)
+            regroup(n, 1, on_vector=True)
+            quantise(n)
+        multiply(d)
+        finish(d)

@@ -44,6 +44,12 @@ def tile_tromptcell_pb_kernel(
         x_rows = const.tile([P, COLUMNS], BF16, name="x_rows")
         nc.scalar.dma_start(out=x_rows[0:SAMPLES, :], in_=x)
         nc.scalar.dma_start(out=x_rows[SAMPLES : 2 * SAMPLES, :], in_=x)
+        rows = const.tile([P, P], BF16, name="rows")
+        nc.vector.memset(rows[:], 0.0)
+        nc.scalar.dma_start(out=rows[0:4, :], in_=ln_emb_w.rearrange("(b d) -> b d", d=P))
+        nc.scalar.dma_start(out=rows[4:8, :], in_=ln_emb_b.rearrange("(b d) -> b d", d=P))
+        nc.scalar.dma_start(out=rows[8:9, :], in_=W_exp.rearrange("(o q) -> o q", o=1))
+        nc.scalar.dma_start(out=rows[9:10, :], in_=b_exp.rearrange("(o q) -> o q", o=1))
         warm = const.tile([P, 1], F32, name="warm")
         nc.gpsimd.memset(warm[:], 1.0)
         nc.scalar.activation(out=warm[:], in_=warm[:], func=ACT.Sqrt)
@@ -56,12 +62,6 @@ def tile_tromptcell_pb_kernel(
         for t in range(PACK):
             nc.sync.dma_start(out=b_sb[t][:], in_=b_view[:, t, :])
             nc.sync.dma_start(out=w_sb[t][:], in_=w_view[:, t, :])
-        rows = const.tile([P, P], BF16, name="rows")
-        nc.vector.memset(rows[:], 0.0)
-        nc.scalar.dma_start(out=rows[0:4, :], in_=ln_emb_w.rearrange("(b d) -> b d", d=P))
-        nc.scalar.dma_start(out=rows[4:8, :], in_=ln_emb_b.rearrange("(b d) -> b d", d=P))
-        nc.scalar.dma_start(out=rows[8:9, :], in_=W_exp.rearrange("(o q) -> o q", o=1))
-        nc.scalar.dma_start(out=rows[9:10, :], in_=b_exp.rearrange("(o q) -> o q", o=1))
         mask_sb = const.tile([P, SAMPLES, COLUMNS], BF16, name="mask_sb")
         for g in range(SAMPLES // MASK_GROUP):
             group = slice(g * MASK_GROUP, (g + 1) * MASK_GROUP)
@@ -87,12 +87,10 @@ def tile_tromptcell_pb_kernel(
         cols_ps = psum.tile([P, P], BF16, name="cols_ps", tag="acc")
         nc.tensor.transpose(cols_ps[:], rows[:], ident_bf[:])
         cols = const.tile([P, 16], F32, name="cols")
-        nc.scalar.copy(out=cols[:], in_=cols_ps[:, 0:16])
         ln_w_col = [cols[:, b : b + 1] for b in range(FEATURE_BLOCKS)]
         ln_b_col = [cols[:, FEATURE_BLOCKS + b : FEATURE_BLOCKS + b + 1] for b in range(FEATURE_BLOCKS)]
         b_exp_col = cols[:, 9:10]
         one_plus_w_exp = const.tile([P, 1], F32, name="one_plus_w_exp")
-        nc.gpsimd.tensor_scalar_add(out=one_plus_w_exp[:], in0=cols[:, 8:9], scalar1=1.0)
 
         mask_words = const.tile([P, SAMPLES, PROMPTS, PAIRS], F32, name="mask_words", align_bytes=64)
         mask_codes = const.tile([P, SAMPLES * PROMPTS], U32, name="mask_codes", align_bytes=64)
@@ -255,6 +253,10 @@ def tile_tromptcell_pb_kernel(
             multiply(n)
             finish(n)
 
+        def take_vectors():
+            nc.scalar.copy(out=cols[:], in_=cols_ps[:, 0:16])
+            nc.gpsimd.tensor_scalar_add(out=one_plus_w_exp[:], in0=cols[:, 8:9], scalar1=1.0)
+
         def row_sums(g):
             for n in range(g * MASK_GROUP, (g + 1) * MASK_GROUP):
                 values = (
@@ -310,6 +312,8 @@ def tile_tromptcell_pb_kernel(
             due(pool, j - 4, SAMPLES)
             due(transpose_mask, j, mask_groups)
             due(row_sums, j, mask_groups)
+            if j == 0:
+                take_vectors()
 
         a, b_, c, d = SAMPLES - 4, SAMPLES - 3, SAMPLES - 2, SAMPLES - 1
         invert(c)

@@ -103,9 +103,10 @@ def tile_tromptcell_pb_kernel(
         act, moments, std, neg_mean, e_t, grouped, total, spread = {}, {}, {}, {}, {}, {}, {}, {}
         rstd, z_t, e_w, codes, scales, acc = {}, {}, {}, {}, {}, {}
 
-        def embed(n):
-            act[n] = work.tile([P, PACK, FEATURES], F32, name="act", bufs=5)
-            for t in range(PACK):
+        def embed(n, groups):
+            if 0 in groups:
+                act[n] = work.tile([P, PACK, FEATURES], F32, name="act", bufs=5)
+            for t in groups:
                 nc.vector.scalar_tensor_tensor(
                     out=act[n][:, t, :],
                     in0=w_sb[t][:],
@@ -114,6 +115,8 @@ def tile_tromptcell_pb_kernel(
                     op0=ALU.mult,
                     op1=ALU.add,
                 )
+
+        def relu(n):
             mine = act[n][:, 0:LAST, :]
             nc.gpsimd.tensor_scalar(out=mine, in0=mine, scalar1=LARGEST_F32, scalar2=0.0, op0=ALU.min, op1=ALU.max)
 
@@ -157,9 +160,9 @@ def tile_tromptcell_pb_kernel(
             rstd[n] = small.tile([P, PACK], F32, name="rstd")
             nc.vector.reciprocal(out=rstd[n][:], in_=std[n][:])
 
-        def normalise(n, on_vector=False):
+        def normalise(n, groups=range(PACK), on_vector=False):
             engine = nc.vector if on_vector else nc.gpsimd
-            for t in range(PACK):
+            for t in groups:
                 engine.tensor_scalar(
                     out=act[n][:, t, :],
                     in0=act[n][:, t, :],
@@ -292,63 +295,109 @@ def tile_tromptcell_pb_kernel(
                 .bitcast(BF16),
             )
 
-        def due(stage, index, count):
-            if 0 <= index < count:
-                stage(index)
+        def due(stage, n, *rest, **how):
+            if 0 <= n < SAMPLES:
+                stage(n, *rest, **how)
 
         mask_groups = SAMPLES // MASK_GROUP
-        for j in range(SAMPLES):
-            due(embed, j, SAMPLES)
-            due(quantise_mask, j - 2, mask_groups)
-            due(invert, j - 2, SAMPLES)
-            due(normalise, j - 2, SAMPLES)
-            due(centre_last, j - 1, SAMPLES)
-            due(to_features, j - 3, SAMPLES)
-            due(square_last, j - 1, SAMPLES)
-            due(to_columns, j - 3, SAMPLES)
-            due(relu_last, j, SAMPLES)
-            due(measure, j - 1, SAMPLES)
-            due(deviation, j - 1, SAMPLES)
-            due(pool, j - 4, SAMPLES)
-            due(transpose_mask, j, mask_groups)
-            due(row_sums, j, mask_groups)
-            if j == 0:
-                take_vectors()
+        for j in range(SAMPLES - 1):
+            due(embed, j, (0,))
+            due(quantise, j - 4)
+            if j % MASK_GROUP == MASK_GROUP - 1:
+                quantise_mask(j // MASK_GROUP)
+            due(invert, j - 2)
+            due(embed, j, (1, 2, 3))
+            due(normalise, j - 2)
+            due(relu, j)
+            due(centre_last, j - 1)
+            due(to_features, j - 3)
+            due(multiply, j - 4)
+            due(square_last, j - 1)
+            due(to_columns, j - 3)
+            due(finish, j - 4)
+            due(relu_last, j)
+            due(measure, j - 1)
+            due(deviation, j - 1)
 
-        a, b_, c, d = SAMPLES - 4, SAMPLES - 3, SAMPLES - 2, SAMPLES - 1
-        invert(c)
-        normalise(c)
-        measure(d)
+            if j == 1:
+                take_vectors()
+            if j < 2:
+                transpose_mask(2 * j)
+                transpose_mask(2 * j + 1)
+            if 2 <= j < 4:
+                row_sums(2 * j - 4)
+                row_sums(2 * j - 3)
+
+        z, a, b_, c, d = range(SAMPLES - 5, SAMPLES)
+        embed(d, (0,))
+        quantise(z)
+        invert(b_)
+        embed(d, (1, 2, 3))
+        normalise(b_)
+        relu(d)
+        centre_last(c)
+        to_features(a)
+        multiply(z)
+        square_last(c)
+        to_columns(a)
+        relu_last(d)
+        measure(c)
+        deviation(c)
         centre_last(d)
         square_last(d)
-        for b in range(2):
-            turn_to_features(b_, b)
-            affine(b_, b)
+        turn_to_features(b_, 0)
+        affine(b_, 0, on_vector=True)
+        invert(c)
+        turn_to_features(b_, 1)
+        affine(b_, 1, on_vector=True)
         turn_to_features(b_, 2)
-        deviation(d)
-        quantise(a)
-        affine(b_, 2, on_vector=True)
+        affine(b_, 2)
         turn_to_features(b_, 3)
-        affine(b_, 3, on_vector=True)
+        affine(b_, 3)
+        normalise(c, on_vector=True)
+        measure(d)
         turn_to_columns(b_, 0)
         regroup(b_, 0)
-        multiply(a)
-        finish(a)
-        invert(d)
-        normalise(d, on_vector=True)
+        finish(z)
+        turn_to_features(c, 0)
         turn_to_columns(b_, 1)
         regroup(b_, 1)
+        affine(c, 0)
+        deviation(d)
+        turn_to_features(c, 1)
+        affine(c, 1)
+        quantise_mask(SAMPLES // MASK_GROUP - 1)
+        quantise(a)
+        invert(d)
+        normalise(d, on_vector=True)
+        turn_to_features(c, 2)
+        affine(c, 2)
         quantise(b_)
-        for n in (c, d):
-            for b in range(FEATURE_BLOCKS):
-                turn_to_features(n, b)
-                affine(n, b, on_vector=(b % 2 == 1))
-            multiply(n - 1)
-            turn_to_columns(n, 0)
-            regroup(n, 0)
-            finish(n - 1)
-            turn_to_columns(n, 1)
-            regroup(n, 1, on_vector=True)
-            quantise(n)
+        turn_to_features(c, 3)
+        affine(c, 3)
+        multiply(a)
+        finish(a)
+        turn_to_features(d, 0)
+        affine(d, 0, on_vector=True)
+        turn_to_columns(c, 0)
+        regroup(c, 0)
+        turn_to_features(d, 1)
+        affine(d, 1)
+        turn_to_columns(c, 1)
+        regroup(c, 1, on_vector=True)
+        quantise(c)
+        multiply(b_)
+        finish(b_)
+        turn_to_features(d, 2)
+        affine(d, 2, on_vector=True)
+        turn_to_features(d, 3)
+        affine(d, 3)
+        turn_to_columns(d, 0)
+        regroup(d, 0)
+        turn_to_columns(d, 1)
+        regroup(d, 1, on_vector=True)
+        multiply(c)
+        finish(c)
+        quantise(d)
         multiply(d)
         finish(d)

@@ -306,8 +306,9 @@ def tile_tromptcell_pb_kernel(
             if j % MASK_GROUP == MASK_GROUP - 1:
                 quantise_mask(j // MASK_GROUP)
             due(invert, j - 2)
+            due(normalise, j - 2, (0,), on_vector=True)
             due(embed, j, (1, 2, 3))
-            due(normalise, j - 2)
+            due(normalise, j - 2, (1, 2, 3))
             due(relu, j)
             due(centre_last, j - 1)
             due(to_features, j - 3)
@@ -332,8 +333,9 @@ def tile_tromptcell_pb_kernel(
         embed(d, (0,))
         quantise(z)
         invert(b_)
+        normalise(b_, (0,), on_vector=True)
         embed(d, (1, 2, 3))
-        normalise(b_)
+        normalise(b_, (1, 2, 3))
         relu(d)
         centre_last(c)
         to_features(a)

@@ -100,6 +100,10 @@ def tile_tromptcell_pb_kernel(
         nc.vector.memset(ones[:], 1.0)
         sums = psum.tile([P, SAMPLES], F32, name="sums", tag="acc")
 
+        minus = const.tile([P, PACK], F32, name="minus")
+        nc.gpsimd.memset(minus[:, 0:LAST], -1.0)
+        nc.gpsimd.memset(minus[:, LAST:PACK], -1.0 / FEATURES)
+
         act, moments, std, neg_mean, e_t, grouped, total, spread = {}, {}, {}, {}, {}, {}, {}, {}
         rstd, z_t, e_w, codes, scales, acc = {}, {}, {}, {}, {}, {}
 
@@ -121,15 +125,9 @@ def tile_tromptcell_pb_kernel(
             nc.gpsimd.tensor_scalar(out=mine, in0=mine, scalar1=LARGEST_F32, scalar2=0.0, op0=ALU.min, op1=ALU.max)
 
         def relu_last(n):
-            total[n] = small.tile([P, 1], F32, name="total")
+            moments[n] = small.tile([P, PACK, 2], F32, name="moments", bufs=4)
             nc.scalar.activation(
-                out=act[n][:, LAST, :], in_=act[n][:, LAST, :], func=ACT.Relu, accum_out=total[n][:]
-            )
-
-        def centre_last(n):
-            neg_mean[n] = small.tile([P, PACK], F32, name="neg_mean")
-            nc.scalar.activation(
-                out=neg_mean[n][:, LAST : LAST + 1], in_=total[n][:], func=ACT.Copy, scale=-1.0 / FEATURES
+                out=act[n][:, LAST, :], in_=act[n][:, LAST, :], func=ACT.Relu, accum_out=moments[n][:, LAST, 0:1]
             )
 
         def square_last(n):
@@ -137,12 +135,11 @@ def tile_tromptcell_pb_kernel(
             spread[n] = small.tile([P, 1], F32, name="spread")
             nc.scalar.activation(
                 out=squares[:], in_=act[n][:, LAST, :], func=ACT.Square,
-                bias=neg_mean[n][:, LAST : LAST + 1], accum_out=spread[n][:],
+                scale=-float(FEATURES), bias=moments[n][:, LAST, 0:1], accum_out=spread[n][:],
             )
 
         def measure(n):
             stats = small.tile([P, LAST, 6], F32, name="stats")
-            moments[n] = small.tile([P, LAST, 2], F32, name="moments")
             for t in range(LAST):
                 nc.vector.bn_stats(out=stats[:, t, :], in_=act[n][:, t, :])
             for t in range(LAST):
@@ -150,26 +147,31 @@ def tile_tromptcell_pb_kernel(
 
         def deviation(n):
             std[n] = small.tile([P, PACK], F32, name="std")
-            nc.scalar.activation(out=std[n][:, 0:LAST], in_=moments[n][:, :, 1], func=ACT.Sqrt, bias=EPS)
+            nc.scalar.activation(out=std[n][:, 0:LAST], in_=moments[n][:, 0:LAST, 1], func=ACT.Sqrt, bias=EPS)
             nc.scalar.activation(
-                out=std[n][:, LAST : LAST + 1], in_=spread[n][:], func=ACT.Sqrt, scale=1.0 / FEATURES, bias=EPS
+                out=std[n][:, LAST : LAST + 1], in_=spread[n][:], func=ACT.Sqrt, scale=1.0 / FEATURES**3, bias=EPS
             )
-            nc.scalar.activation(out=neg_mean[n][:, 0:LAST], in_=moments[n][:, :, 0], func=ACT.Copy, scale=-1.0)
+
+        def negate(n):
+            neg_mean[n] = small.tile([P, PACK], F32, name="neg_mean")
+            nc.vector.tensor_tensor(out=neg_mean[n][:], in0=moments[n][:, :, 0], in1=minus[:], op=ALU.mult)
 
         def invert(n):
             rstd[n] = small.tile([P, PACK], F32, name="rstd")
             nc.vector.reciprocal(out=rstd[n][:], in_=std[n][:])
 
-        def normalise(n, groups=range(PACK), on_vector=False):
+        def normalise_first(n):
+            nc.vector.tensor_scalar(
+                out=act[n][:, 0, :], in0=act[n][:, 0, :], scalar1=moments[n][:, 0, 0:1], scalar2=rstd[n][:, 0:1],
+                op0=ALU.subtract, op1=ALU.mult,
+            )
+
+        def normalise_rest(n, on_vector=False):
             engine = nc.vector if on_vector else nc.gpsimd
-            for t in groups:
+            for t in range(1, PACK):
                 engine.tensor_scalar(
-                    out=act[n][:, t, :],
-                    in0=act[n][:, t, :],
-                    scalar1=neg_mean[n][:, t : t + 1],
-                    scalar2=rstd[n][:, t : t + 1],
-                    op0=ALU.add,
-                    op1=ALU.mult,
+                    out=act[n][:, t, :], in0=act[n][:, t, :], scalar1=neg_mean[n][:, t : t + 1],
+                    scalar2=rstd[n][:, t : t + 1], op0=ALU.add, op1=ALU.mult,
                 )
 
         def turn_to_features(n, b):
@@ -285,14 +287,12 @@ def tile_tromptcell_pb_kernel(
                     out=mask_words[:, first : first + 2, :, :], in_=m_t[:].rearrange("p s u q -> p s q u")
                 )
 
-        def quantise_mask(g):
-            prompts = slice(g * MASK_GROUP * PROMPTS, (g + 1) * MASK_GROUP * PROMPTS)
+        def quantise_mask(n):
+            prompts = slice(n * PROMPTS, (n + 1) * PROMPTS)
             nc.vector.quantize_mx(
                 out=mask_codes[:, prompts].bitcast(FP8X4),
                 scales=mask_scales[:, prompts],
-                in_=mask_words[:, g * MASK_GROUP : (g + 1) * MASK_GROUP, :, :]
-                .rearrange("p n q u -> p (n q u)")
-                .bitcast(BF16),
+                in_=mask_words[:, n, :, :].rearrange("p q u -> p (q u)").bitcast(BF16),
             )
 
         def due(stage, n, *rest, **how):
@@ -303,14 +303,13 @@ def tile_tromptcell_pb_kernel(
         for j in range(SAMPLES - 1):
             due(embed, j, (0,))
             due(quantise, j - 4)
-            if j % MASK_GROUP == MASK_GROUP - 1:
-                quantise_mask(j // MASK_GROUP)
             due(invert, j - 2)
-            due(normalise, j - 2, (0,), on_vector=True)
+            due(negate, j - 2)
+            due(quantise_mask, j - 3)
+            due(normalise_first, j - 2)
             due(embed, j, (1, 2, 3))
-            due(normalise, j - 2, (1, 2, 3))
+            due(normalise_rest, j - 2)
             due(relu, j)
-            due(centre_last, j - 1)
             due(to_features, j - 3)
             due(multiply, j - 4)
             due(square_last, j - 1)
@@ -319,7 +318,6 @@ def tile_tromptcell_pb_kernel(
             due(relu_last, j)
             due(measure, j - 1)
             due(deviation, j - 1)
-
             if j == 1:
                 take_vectors()
             if j < 2:
@@ -333,11 +331,12 @@ def tile_tromptcell_pb_kernel(
         embed(d, (0,))
         quantise(z)
         invert(b_)
-        normalise(b_, (0,), on_vector=True)
+        negate(b_)
+        quantise_mask(a)
+        normalise_first(b_)
         embed(d, (1, 2, 3))
-        normalise(b_, (1, 2, 3))
+        normalise_rest(b_)
         relu(d)
-        centre_last(c)
         to_features(a)
         multiply(z)
         square_last(c)
@@ -345,18 +344,19 @@ def tile_tromptcell_pb_kernel(
         relu_last(d)
         measure(c)
         deviation(c)
-        centre_last(d)
         square_last(d)
         turn_to_features(b_, 0)
         affine(b_, 0, on_vector=True)
         invert(c)
+        negate(c)
         turn_to_features(b_, 1)
         affine(b_, 1, on_vector=True)
         turn_to_features(b_, 2)
         affine(b_, 2)
         turn_to_features(b_, 3)
         affine(b_, 3)
-        normalise(c, on_vector=True)
+        normalise_first(c)
+        normalise_rest(c, on_vector=True)
         measure(d)
         turn_to_columns(b_, 0)
         regroup(b_, 0)
@@ -368,10 +368,13 @@ def tile_tromptcell_pb_kernel(
         deviation(d)
         turn_to_features(c, 1)
         affine(c, 1)
-        quantise_mask(SAMPLES // MASK_GROUP - 1)
+        quantise_mask(b_)
         quantise(a)
         invert(d)
-        normalise(d, on_vector=True)
+        negate(d)
+        quantise_mask(c)
+        normalise_first(d)
+        normalise_rest(d, on_vector=True)
         turn_to_features(c, 2)
         affine(c, 2)
         quantise(b_)
@@ -387,6 +390,7 @@ def tile_tromptcell_pb_kernel(
         affine(d, 1)
         turn_to_columns(c, 1)
         regroup(c, 1, on_vector=True)
+        quantise_mask(d)
         quantise(c)
         multiply(b_)
         finish(b_)

@@ -115,7 +115,7 @@ def tile_tromptcell_pb_kernel(
                     out=act[n][:, t, :],
                     in0=w_sb[t][:],
                     scalar=x_sb[:, n, t : t + 1],
-                    in1=bias_ps[t // 2][:, t % 2, :],
+                    in1=b_sb[t][:] if n == 0 else bias_ps[t // 2][:, t % 2, :],
                     op0=ALU.mult,
                     op1=ALU.add,
                 )
@@ -166,9 +166,9 @@ def tile_tromptcell_pb_kernel(
                 op0=ALU.subtract, op1=ALU.mult,
             )
 
-        def normalise_rest(n, on_vector=False):
+        def normalise(n, groups, on_vector=False):
             engine = nc.vector if on_vector else nc.gpsimd
-            for t in range(1, PACK):
+            for t in groups:
                 engine.tensor_scalar(
                     out=act[n][:, t, :], in0=act[n][:, t, :], scalar1=neg_mean[n][:, t : t + 1],
                     scalar2=rstd[n][:, t : t + 1], op0=ALU.add, op1=ALU.mult,
@@ -210,38 +210,45 @@ def tile_tromptcell_pb_kernel(
             else:
                 nc.scalar.copy(out=target, in_=source)
 
-        def quantise(n):
-            codes[n] = work.tile([P, FEATURES], U32, name="codes", align_bytes=64)
-            scales[n] = work.tile([P, FEATURES], U8, name="scales", align_bytes=64)
+        def quantise(n, first=0, last=FEATURES):
+            if first == 0:
+                codes[n] = work.tile([P, FEATURES], U32, name="codes", align_bytes=64)
+                scales[n] = work.tile([P, FEATURES], U8, name="scales", align_bytes=64)
             nc.vector.quantize_mx(
-                out=codes[n][:].bitcast(FP8X4),
-                scales=scales[n][:],
-                in_=grouped[n][:].rearrange("p d u -> p (d u)").bitcast(BF16),
+                out=codes[n][:, first:last].bitcast(FP8X4),
+                scales=scales[n][:, first:last],
+                in_=grouped[n][:, first:last, :].rearrange("p d u -> p (d u)").bitcast(BF16),
             )
 
-        def multiply(n):
+        def multiply(n, first=0, last=FEATURES):
             prompts = slice(n * PROMPTS, (n + 1) * PROMPTS)
-            acc[n] = psum.tile([P, FEATURES], F32, name="acc", tag="acc")
+            if first == 0:
+                acc[n] = psum.tile([P, FEATURES], F32, name="acc", tag="acc")
+            else:
+                acc[n] = psum.tile([P, FEATURES], F32, name="acc_end", tag="z_t", bufs=3)
             nc.tensor.matmul_mx(
-                out=acc[n][:],
+                out=acc[n][:, first:last],
                 lhsT=mask_codes[:, prompts].bitcast(FP8X4),
                 lhsT_scale=mask_scales[:, prompts],
-                rhs=codes[n][:].bitcast(FP8X4),
-                rhs_scale=scales[n][:],
+                rhs=codes[n][:, first:last].bitcast(FP8X4),
+                rhs_scale=scales[n][:, first:last],
                 start=True,
                 stop=True,
             )
 
-        def finish(n):
+        def finish(n, first=0, last=FEATURES, on_vector=False):
             result = work.tile([P, FEATURES], F32, name="result", bufs=3)
-            nc.scalar.activation(
-                out=result[:],
-                in_=acc[n][:],
-                func=ACT.Identity,
-                scale=one_plus_w_exp[:, 0:1],
-                bias=out_bias[:, n : n + 1],
-            )
-            nc.sync.dma_start(out=out[n], in_=result[:])
+            scale, bias = one_plus_w_exp[:, 0:1], out_bias[:, n : n + 1]
+            if on_vector:
+                nc.vector.tensor_scalar(
+                    out=result[:, first:last], in0=acc[n][:, first:last], scalar1=scale, scalar2=bias,
+                    op0=ALU.mult, op1=ALU.add,
+                )
+            else:
+                nc.scalar.activation(
+                    out=result[:, first:last], in_=acc[n][:, first:last], func=ACT.Identity, scale=scale, bias=bias
+                )
+            nc.sync.dma_start(out=out[n, :, first:last], in_=result[:, first:last])
 
         def to_features(n):
             for b in range(FEATURE_BLOCKS):
@@ -306,9 +313,10 @@ def tile_tromptcell_pb_kernel(
             due(invert, j - 2)
             due(negate, j - 2)
             due(quantise_mask, j - 3)
-            due(normalise_first, j - 2)
+            if j > 2:
+                due(normalise_first, j - 2)
             due(embed, j, (1, 2, 3))
-            due(normalise_rest, j - 2)
+            due(normalise, j - 2, range(0 if j == 2 else 1, PACK))
             due(relu, j)
             due(to_features, j - 3)
             due(multiply, j - 4)
@@ -335,7 +343,7 @@ def tile_tromptcell_pb_kernel(
         quantise_mask(a)
         normalise_first(b_)
         embed(d, (1, 2, 3))
-        normalise_rest(b_)
+        normalise(b_, (1, 2, 3))
         relu(d)
         to_features(a)
         multiply(z)
@@ -356,16 +364,16 @@ def tile_tromptcell_pb_kernel(
         turn_to_features(b_, 3)
         affine(b_, 3)
         normalise_first(c)
-        normalise_rest(c, on_vector=True)
+        normalise(c, (1, 2, 3))
         measure(d)
         turn_to_columns(b_, 0)
         regroup(b_, 0)
         finish(z)
-        turn_to_features(c, 0)
         turn_to_columns(b_, 1)
         regroup(b_, 1)
-        affine(c, 0)
         deviation(d)
+        turn_to_features(c, 0)
+        affine(c, 0)
         turn_to_features(c, 1)
         affine(c, 1)
         quantise_mask(b_)
@@ -374,7 +382,7 @@ def tile_tromptcell_pb_kernel(
         negate(d)
         quantise_mask(c)
         normalise_first(d)
-        normalise_rest(d, on_vector=True)
+        normalise(d, (1, 2, 3), on_vector=True)
         turn_to_features(c, 2)
         affine(c, 2)
         quantise(b_)
@@ -400,10 +408,13 @@ def tile_tromptcell_pb_kernel(
         affine(d, 3)
         turn_to_columns(d, 0)
         regroup(d, 0)
+        quantise(d, 0, HALF)
         turn_to_columns(d, 1)
         regroup(d, 1, on_vector=True)
+        quantise(d, HALF, FEATURES)
         multiply(c)
         finish(c)
-        quantise(d)
-        multiply(d)
-        finish(d)
+        multiply(d, 0, HALF)
+        finish(d, 0, HALF)
+        multiply(d, HALF, FEATURES)
+        finish(d, HALF, FEATURES, on_vector=True)

@@ -42,6 +42,8 @@ def tile_tromptcell_pb_kernel(
         ctx.enter_context(tc.manual_schedule())
 
         x_rows = const.tile([P, COLUMNS], BF16, name="x_rows")
+        x_first = const.tile([P, PACK], BF16, name="x_first")
+        nc.scalar.dma_start(out=x_first[:], in_=x[0].rearrange("(p t) -> p t", t=PACK))
         nc.scalar.dma_start(out=x_rows[0:SAMPLES, :], in_=x)
         nc.scalar.dma_start(out=x_rows[SAMPLES : 2 * SAMPLES, :], in_=x)
         rows = const.tile([P, P], BF16, name="rows")
@@ -59,7 +61,7 @@ def tile_tromptcell_pb_kernel(
         w_view = feature_emb_weight.rearrange("(p t) d -> p t d", t=PACK)
         b_sb = [const.tile([P, FEATURES], BF16, name="b_sb%d" % t) for t in range(PACK)]
         w_sb = [const.tile([P, FEATURES], BF16, name="w_sb%d" % t) for t in range(PACK)]
-        for t in range(PACK):
+        for t in (2, LAST, 0, 1):
             nc.sync.dma_start(out=b_sb[t][:], in_=b_view[:, t, :])
             nc.sync.dma_start(out=w_sb[t][:], in_=w_view[:, t, :])
         mask_sb = const.tile([P, SAMPLES, COLUMNS], BF16, name="mask_sb")
@@ -76,7 +78,6 @@ def tile_tromptcell_pb_kernel(
         for t in range(PACK):
             nc.tensor.transpose(x_ps[:, t, :], x_rows[:].rearrange("n (p t) -> n t p", t=PACK)[:, t, :], ident_bf[:])
         x_sb = const.tile([P, SAMPLES, PACK], BF16, name="x_sb")
-        nc.vector.tensor_copy(out=x_sb[:], in_=x_ps[:, :, 0:SAMPLES].rearrange("p t n -> p n t"))
 
         bias_ps = [psum_const.tile([P, 2, FEATURES], BF16, name="bias_ps%d" % h) for h in range(2)]
         for t in range(PACK):
@@ -100,61 +101,75 @@ def tile_tromptcell_pb_kernel(
         nc.vector.memset(ones[:], 1.0)
         sums = psum.tile([P, SAMPLES], F32, name="sums", tag="acc")
 
-        minus = const.tile([P, PACK], F32, name="minus")
-        nc.gpsimd.memset(minus[:, 0:LAST], -1.0)
-        nc.gpsimd.memset(minus[:, LAST:PACK], -1.0 / FEATURES)
+        def first_scalar(n):
+            return LAST - 1 if n == 0 else LAST
 
-        act, moments, std, neg_mean, e_t, grouped, total, spread = {}, {}, {}, {}, {}, {}, {}, {}
+        minus = {}
+        for first in (LAST - 1, LAST):
+            minus[first] = const.tile([P, PACK], F32, name="minus%d" % first)
+            nc.gpsimd.memset(minus[first][:, 0:first], -1.0)
+            nc.gpsimd.memset(minus[first][:, first:PACK], -1.0 / FEATURES)
+
+        act, stats, moments, std, neg_mean, e_t, grouped, total, spread = {}, {}, {}, {}, {}, {}, {}, {}, {}
         rstd, z_t, e_w, codes, scales, acc = {}, {}, {}, {}, {}, {}
 
-        def embed(n, groups):
-            if 0 in groups:
+        def embed(n, groups, first=0, last=FEATURES):
+            if n not in act:
                 act[n] = work.tile([P, PACK, FEATURES], F32, name="act", bufs=5)
             for t in groups:
                 nc.vector.scalar_tensor_tensor(
-                    out=act[n][:, t, :],
-                    in0=w_sb[t][:],
-                    scalar=x_sb[:, n, t : t + 1],
-                    in1=b_sb[t][:] if n == 0 else bias_ps[t // 2][:, t % 2, :],
+                    out=act[n][:, t, first:last],
+                    in0=w_sb[t][:, first:last],
+                    scalar=x_first[:, t : t + 1] if n == 0 else x_sb[:, n, t : t + 1],
+                    in1=b_sb[t][:, first:last] if n == 0 else bias_ps[t // 2][:, t % 2, first:last],
                     op0=ALU.mult,
                     op1=ALU.add,
                 )
 
         def relu(n):
-            mine = act[n][:, 0:LAST, :]
+            mine = act[n][:, 0 : first_scalar(n), :]
             nc.gpsimd.tensor_scalar(out=mine, in0=mine, scalar1=LARGEST_F32, scalar2=0.0, op0=ALU.min, op1=ALU.max)
 
         def relu_last(n):
             moments[n] = small.tile([P, PACK, 2], F32, name="moments", bufs=4)
-            nc.scalar.activation(
-                out=act[n][:, LAST, :], in_=act[n][:, LAST, :], func=ACT.Relu, accum_out=moments[n][:, LAST, 0:1]
-            )
+            for t in range(first_scalar(n), PACK):
+                nc.scalar.activation(
+                    out=act[n][:, t, :], in_=act[n][:, t, :], func=ACT.Relu, accum_out=moments[n][:, t, 0:1]
+                )
 
         def square_last(n):
-            squares = work.tile([P, FEATURES], BF16, name="squares")
-            spread[n] = small.tile([P, 1], F32, name="spread")
-            nc.scalar.activation(
-                out=squares[:], in_=act[n][:, LAST, :], func=ACT.Square,
-                scale=-float(FEATURES), bias=moments[n][:, LAST, 0:1], accum_out=spread[n][:],
-            )
+            for t in range(first_scalar(n), PACK):
+                squares = work.tile([P, FEATURES], BF16, name="squares")
+                nc.scalar.activation(
+                    out=squares[:], in_=act[n][:, t, :], func=ACT.Square,
+                    scale=-float(FEATURES), bias=moments[n][:, t, 0:1], accum_out=moments[n][:, t, 1:2],
+                )
 
         def measure(n):
-            stats = small.tile([P, LAST, 6], F32, name="stats")
-            for t in range(LAST):
-                nc.vector.bn_stats(out=stats[:, t, :], in_=act[n][:, t, :])
-            for t in range(LAST):
-                nc.vector.bn_aggr(out=moments[n][:, t, :], in_=stats[:, t, :])
+            stats[n] = small.tile([P, LAST, 6], F32, name="stats")
+            for t in range(first_scalar(n)):
+                nc.vector.bn_stats(out=stats[n][:, t, :], in_=act[n][:, t, :])
+            for t in range(first_scalar(n) - 1):
+                nc.vector.bn_aggr(out=moments[n][:, t, :], in_=stats[n][:, t, :])
+
+        def measure_end(n):
+            t = first_scalar(n) - 1
+            nc.vector.bn_aggr(out=moments[n][:, t, :], in_=stats[n][:, t, :])
 
         def deviation(n):
             std[n] = small.tile([P, PACK], F32, name="std")
-            nc.scalar.activation(out=std[n][:, 0:LAST], in_=moments[n][:, 0:LAST, 1], func=ACT.Sqrt, bias=EPS)
+            first = first_scalar(n)
+            nc.scalar.activation(out=std[n][:, 0:first], in_=moments[n][:, 0:first, 1], func=ACT.Sqrt, bias=EPS)
             nc.scalar.activation(
-                out=std[n][:, LAST : LAST + 1], in_=spread[n][:], func=ACT.Sqrt, scale=1.0 / FEATURES**3, bias=EPS
+                out=std[n][:, first:PACK], in_=moments[n][:, first:PACK, 1], func=ACT.Sqrt,
+                scale=1.0 / FEATURES**3, bias=EPS,
             )
 
         def negate(n):
             neg_mean[n] = small.tile([P, PACK], F32, name="neg_mean")
-            nc.vector.tensor_tensor(out=neg_mean[n][:], in0=moments[n][:, :, 0], in1=minus[:], op=ALU.mult)
+            nc.vector.tensor_tensor(
+                out=neg_mean[n][:], in0=moments[n][:, :, 0], in1=minus[first_scalar(n)][:], op=ALU.mult
+            )
 
         def invert(n):
             rstd[n] = small.tile([P, PACK], F32, name="rstd")
@@ -212,20 +227,20 @@ def tile_tromptcell_pb_kernel(
 
         def quantise(n, first=0, last=FEATURES):
             if first == 0:
-                codes[n] = work.tile([P, FEATURES], U32, name="codes", align_bytes=64)
-                scales[n] = work.tile([P, FEATURES], U8, name="scales", align_bytes=64)
+                codes[n] = work.tile([P, FEATURES], U32, name="codes", bufs=3, align_bytes=64)
+                scales[n] = work.tile([P, FEATURES], U8, name="scales", bufs=3, align_bytes=64)
             nc.vector.quantize_mx(
                 out=codes[n][:, first:last].bitcast(FP8X4),
                 scales=scales[n][:, first:last],
                 in_=grouped[n][:, first:last, :].rearrange("p d u -> p (d u)").bitcast(BF16),
             )
 
-        def multiply(n, first=0, last=FEATURES):
+        def multiply(n, first=0, last=FEATURES, in_drain=False):
             prompts = slice(n * PROMPTS, (n + 1) * PROMPTS)
-            if first == 0:
-                acc[n] = psum.tile([P, FEATURES], F32, name="acc", tag="acc")
-            else:
+            if in_drain:
                 acc[n] = psum.tile([P, FEATURES], F32, name="acc_end", tag="z_t", bufs=3)
+            else:
+                acc[n] = psum.tile([P, FEATURES], F32, name="acc", tag="acc")
             nc.tensor.matmul_mx(
                 out=acc[n][:, first:last],
                 lhsT=mask_codes[:, prompts].bitcast(FP8X4),
@@ -237,7 +252,7 @@ def tile_tromptcell_pb_kernel(
             )
 
         def finish(n, first=0, last=FEATURES, on_vector=False):
-            result = work.tile([P, FEATURES], F32, name="result", bufs=3)
+            result = work.tile([P, FEATURES], F32, name="result", bufs=5)
             scale, bias = one_plus_w_exp[:, 0:1], out_bias[:, n : n + 1]
             if on_vector:
                 nc.vector.tensor_scalar(
@@ -307,24 +322,35 @@ def tile_tromptcell_pb_kernel(
                 stage(n, *rest, **how)
 
         mask_groups = SAMPLES // MASK_GROUP
+        embed(0, (2, LAST, 0))
+        nc.vector.tensor_copy(out=x_sb[:], in_=x_ps[:, :, 0:SAMPLES].rearrange("p t n -> p n t"))
+        embed(0, (1,))
+        relu_last(0)
+        square_last(0)
         for j in range(SAMPLES - 1):
-            due(embed, j, (0,))
+            if j > 0:
+                embed(j, (0,), 64, FEATURES)
             due(quantise, j - 4)
             due(invert, j - 2)
             due(negate, j - 2)
             due(quantise_mask, j - 3)
             if j > 2:
                 due(normalise_first, j - 2)
-            due(embed, j, (1, 2, 3))
+            if j > 0:
+                embed(j, (1, 2, 3))
             due(normalise, j - 2, range(0 if j == 2 else 1, PACK))
             due(relu, j)
             due(to_features, j - 3)
-            due(multiply, j - 4)
-            due(square_last, j - 1)
+            if j > 1:
+                square_last(j - 1)
             due(to_columns, j - 3)
+            due(multiply, j - 4)
             due(finish, j - 4)
-            due(relu_last, j)
+            if j > 0:
+                relu_last(j)
             due(measure, j - 1)
+            embed(j + 1, (0,), 0, 64)
+            due(measure_end, j - 1)
             due(deviation, j - 1)
             if j == 1:
                 take_vectors()
@@ -336,7 +362,7 @@ def tile_tromptcell_pb_kernel(
                 row_sums(2 * j - 3)
 
         z, a, b_, c, d = range(SAMPLES - 5, SAMPLES)
-        embed(d, (0,))
+        embed(d, (0,), 64, FEATURES)
         quantise(z)
         invert(b_)
         negate(b_)
@@ -351,6 +377,7 @@ def tile_tromptcell_pb_kernel(
         to_columns(a)
         relu_last(d)
         measure(c)
+        measure_end(c)
         deviation(c)
         square_last(d)
         turn_to_features(b_, 0)
@@ -366,6 +393,7 @@ def tile_tromptcell_pb_kernel(
         normalise_first(c)
         normalise(c, (1, 2, 3))
         measure(d)
+        measure_end(d)
         turn_to_columns(b_, 0)
         regroup(b_, 0)
         finish(z)
@@ -398,23 +426,23 @@ def tile_tromptcell_pb_kernel(
         affine(d, 1)
         turn_to_columns(c, 1)
         regroup(c, 1, on_vector=True)
-        quantise_mask(d)
-        quantise(c)
-        multiply(b_)
-        finish(b_)
         turn_to_features(d, 2)
         affine(d, 2, on_vector=True)
         turn_to_features(d, 3)
         affine(d, 3)
+        quantise_mask(d)
+        quantise(c)
         turn_to_columns(d, 0)
         regroup(d, 0)
-        quantise(d, 0, HALF)
         turn_to_columns(d, 1)
         regroup(d, 1, on_vector=True)
-        quantise(d, HALF, FEATURES)
-        multiply(c)
+        multiply(b_)
+        finish(b_)
+        quantise(d, 0, HALF)
+        multiply(c, in_drain=True)
         finish(c)
-        multiply(d, 0, HALF)
+        quantise(d, HALF, FEATURES)
+        multiply(d, 0, HALF, in_drain=True)
         finish(d, 0, HALF)
-        multiply(d, HALF, FEATURES)
+        multiply(d, HALF, FEATURES, in_drain=True)
         finish(d, HALF, FEATURES, on_vector=True)

@@ -57,6 +57,11 @@ def tile_tromptcell_pb_kernel(
         nc.scalar.activation(out=warm[:], in_=warm[:], func=ACT.Sqrt)
         nc.vector.memset(x_rows[32:64, :], 0.0)
         nc.vector.memset(x_rows[64:128, :], 0.0)
+        minus = {}
+        for first in (LAST - 1, LAST):
+            minus[first] = const.tile([P, PACK], F32, name="minus%d" % first)
+            nc.vector.memset(minus[first][:, 0:first], -1.0)
+            nc.vector.memset(minus[first][:, first:PACK], -1.0 / FEATURES)
         b_view = feature_emb_bias.rearrange("(p t) d -> p t d", t=PACK)
         w_view = feature_emb_weight.rearrange("(p t) d -> p t d", t=PACK)
         b_sb = [const.tile([P, FEATURES], BF16, name="b_sb%d" % t) for t in range(PACK)]
@@ -102,13 +107,7 @@ def tile_tromptcell_pb_kernel(
         sums = psum.tile([P, SAMPLES], F32, name="sums", tag="acc")
 
         def first_scalar(n):
-            return LAST - 1 if n == 0 else LAST
-
-        minus = {}
-        for first in (LAST - 1, LAST):
-            minus[first] = const.tile([P, PACK], F32, name="minus%d" % first)
-            nc.gpsimd.memset(minus[first][:, 0:first], -1.0)
-            nc.gpsimd.memset(minus[first][:, first:PACK], -1.0 / FEATURES)
+            return LAST - 1 if n in (0, 2) else LAST
 
         act, stats, moments, std, neg_mean, e_t, grouped, total, spread = {}, {}, {}, {}, {}, {}, {}, {}, {}
         rstd, z_t, e_w, codes, scales, acc = {}, {}, {}, {}, {}, {}
@@ -325,39 +324,44 @@ def tile_tromptcell_pb_kernel(
         embed(0, (2, LAST, 0))
         nc.vector.tensor_copy(out=x_sb[:], in_=x_ps[:, :, 0:SAMPLES].rearrange("p t n -> p n t"))
         embed(0, (1,))
+        relu(0)
         relu_last(0)
         square_last(0)
-        for j in range(SAMPLES - 1):
-            if j > 0:
-                embed(j, (0,), 64, FEATURES)
+        transpose_mask(0)
+        transpose_mask(1)
+        embed(1, range(PACK))
+        relu(1)
+        measure(0)
+        embed(2, (0,), 0, 64)
+        measure_end(0)
+        relu_last(1)
+        deviation(0)
+        take_vectors()
+        transpose_mask(2)
+        transpose_mask(3)
+
+        for j in range(2, SAMPLES - 1):
+            embed(j, (0,), 64, FEATURES)
             due(quantise, j - 4)
-            due(invert, j - 2)
-            due(negate, j - 2)
+            invert(j - 2)
+            negate(j - 2)
             due(quantise_mask, j - 3)
             if j > 2:
-                due(normalise_first, j - 2)
-            if j > 0:
-                embed(j, (1, 2, 3))
-            due(normalise, j - 2, range(0 if j == 2 else 1, PACK))
-            due(relu, j)
+                normalise_first(j - 2)
+            embed(j, (1, 2, 3))
+            normalise(j - 2, range(0 if j == 2 else 1, PACK))
+            relu(j)
             due(to_features, j - 3)
-            if j > 1:
-                square_last(j - 1)
+            square_last(j - 1)
             due(to_columns, j - 3)
             due(multiply, j - 4)
             due(finish, j - 4)
-            if j > 0:
-                relu_last(j)
-            due(measure, j - 1)
+            relu_last(j)
+            measure(j - 1)
             embed(j + 1, (0,), 0, 64)
-            due(measure_end, j - 1)
-            due(deviation, j - 1)
-            if j == 1:
-                take_vectors()
-            if j < 2:
-                transpose_mask(2 * j)
-                transpose_mask(2 * j + 1)
-            if 2 <= j < 4:
+            measure_end(j - 1)
+            deviation(j - 1)
+            if j < 4:
                 row_sums(2 * j - 4)
                 row_sums(2 * j - 3)
 
@@ -372,52 +376,52 @@ def tile_tromptcell_pb_kernel(
         normalise(b_, (1, 2, 3))
         relu(d)
         to_features(a)
-        multiply(z)
         square_last(c)
         to_columns(a)
+        multiply(z)
         relu_last(d)
+        finish(z)
         measure(c)
         measure_end(c)
         deviation(c)
-        square_last(d)
+
         turn_to_features(b_, 0)
         affine(b_, 0, on_vector=True)
+        quantise(a)
         invert(c)
         negate(c)
-        turn_to_features(b_, 1)
-        affine(b_, 1, on_vector=True)
-        turn_to_features(b_, 2)
-        affine(b_, 2)
-        turn_to_features(b_, 3)
-        affine(b_, 3)
+        quantise_mask(b_)
         normalise_first(c)
         normalise(c, (1, 2, 3))
+        for b in (1, 2, 3):
+            turn_to_features(b_, b)
+            affine(b_, b)
+        square_last(d)
         measure(d)
         measure_end(d)
         turn_to_columns(b_, 0)
         regroup(b_, 0)
-        finish(z)
         turn_to_columns(b_, 1)
         regroup(b_, 1)
+        multiply(a)
         deviation(d)
+        finish(a)
         turn_to_features(c, 0)
         affine(c, 0)
         turn_to_features(c, 1)
         affine(c, 1)
-        quantise_mask(b_)
-        quantise(a)
+        quantise_mask(c)
+        quantise(b_)
         invert(d)
         negate(d)
-        quantise_mask(c)
+        quantise_mask(d)
         normalise_first(d)
         normalise(d, (1, 2, 3), on_vector=True)
         turn_to_features(c, 2)
         affine(c, 2)
-        quantise(b_)
         turn_to_features(c, 3)
         affine(c, 3)
-        multiply(a)
-        finish(a)
+
         turn_to_features(d, 0)
         affine(d, 0, on_vector=True)
         turn_to_columns(c, 0)
@@ -430,7 +434,6 @@ def tile_tromptcell_pb_kernel(
         affine(d, 2, on_vector=True)
         turn_to_features(d, 3)
         affine(d, 3)
-        quantise_mask(d)
         quantise(c)
         turn_to_columns(d, 0)
         regroup(d, 0)

@@ -109,6 +109,10 @@ def tile_tromptcell_pb_kernel(
         def first_scalar(n):
             return LAST - 1 if n in (0, 2) else LAST
 
+        row_w = const.tile([P, FEATURES], BF16, name="row_w")
+        row_b = const.tile([P, FEATURES], BF16, name="row_b")
+        flat = const.tile([P, PACK, FEATURES], BF16, name="flat")
+
         act, stats, moments, std, neg_mean, e_t, grouped, total, spread = {}, {}, {}, {}, {}, {}, {}, {}, {}
         rstd, z_t, e_w, codes, scales, acc = {}, {}, {}, {}, {}, {}
 
@@ -174,6 +178,46 @@ def tile_tromptcell_pb_kernel(
             rstd[n] = small.tile([P, PACK], F32, name="rstd")
             nc.vector.reciprocal(out=rstd[n][:], in_=std[n][:])
 
+        def load_rows():
+            for vector, tile in ((ln_emb_w, row_w), (ln_emb_b, row_b)):
+                nc.sync.dma_start(out=tile[:], in_=vector.partition_broadcast(P))
+
+        def rows_to_psum():
+            rows_ps = psum_const.tile([P, 2, FEATURES], BF16, name="bias_ps0")
+            for k, tile in ((0, row_w), (1, row_b)):
+                nc.tensor.matmul(out=rows_ps[:, k, :], lhsT=ident_bf[:], rhs=tile[:], start=True, stop=True)
+            return rows_ps
+
+        def norm_first_half(n, groups, rows_ps):
+            for t in groups:
+                nc.vector.scalar_tensor_tensor(
+                    out=act[n][:, t, :], in0=act[n][:, t, :], scalar=neg_mean[n][:, t : t + 1],
+                    in1=rows_ps[:, 0, :], op0=ALU.add, op1=ALU.mult,
+                )
+
+        def norm_second_half(n, groups, rows_ps):
+            for t in groups:
+                nc.vector.scalar_tensor_tensor(
+                    out=flat[:, t, :], in0=act[n][:, t, :], scalar=rstd[n][:, t : t + 1],
+                    in1=rows_ps[:, 1, :], op0=ALU.mult, op1=ALU.add,
+                )
+
+        def norm_gpsimd(n, t):
+            normalise(n, (t,))
+            nc.gpsimd.tensor_tensor(out=act[n][:, t, :], in0=act[n][:, t, :], in1=row_w[:], op=ALU.mult)
+            nc.gpsimd.tensor_tensor(out=flat[:, t, :], in0=act[n][:, t, :], in1=row_b[:], op=ALU.add)
+
+        def interleave(n, h, on_scalar=False):
+            if h == 0:
+                grouped[n] = work.tile([P, FEATURES, PAIRS], F32, name="grouped", align_bytes=64)
+            mine = slice(h * HALF, (h + 1) * HALF)
+            target = grouped[n][:].rearrange("p d u -> p (d u)").bitcast(BF16).rearrange("p (d t) -> p d t", t=PACK)[:, mine, :]
+            source = flat[:].rearrange("p t d -> p d t")[:, mine, :]
+            if on_scalar:
+                nc.scalar.copy(out=target, in_=source)
+            else:
+                nc.vector.tensor_copy(out=target, in_=source)
+
         def normalise_first(n):
             nc.vector.tensor_scalar(
                 out=act[n][:, 0, :], in0=act[n][:, 0, :], scalar1=moments[n][:, 0, 0:1], scalar2=rstd[n][:, 0:1],
@@ -226,8 +270,8 @@ def tile_tromptcell_pb_kernel(
 
         def quantise(n, first=0, last=FEATURES):
             if first == 0:
-                codes[n] = work.tile([P, FEATURES], U32, name="codes", bufs=3, align_bytes=64)
-                scales[n] = work.tile([P, FEATURES], U8, name="scales", bufs=3, align_bytes=64)
+                codes[n] = work.tile([P, FEATURES], U32, name="codes", bufs=4, align_bytes=64)
+                scales[n] = work.tile([P, FEATURES], U8, name="scales", bufs=4, align_bytes=64)
             nc.vector.quantize_mx(
                 out=codes[n][:, first:last].bitcast(FP8X4),
                 scales=scales[n][:, first:last],
@@ -251,7 +295,7 @@ def tile_tromptcell_pb_kernel(
             )
 
         def finish(n, first=0, last=FEATURES, on_vector=False):
-            result = work.tile([P, FEATURES], F32, name="result", bufs=5)
+            result = work.tile([P, FEATURES], F32, name="result", bufs=6)
             scale, bias = one_plus_w_exp[:, 0:1], out_bias[:, n : n + 1]
             if on_vector:
                 nc.vector.tensor_scalar(
@@ -361,6 +405,8 @@ def tile_tromptcell_pb_kernel(
             embed(j + 1, (0,), 0, 64)
             measure_end(j - 1)
             deviation(j - 1)
+            if j == 4:
+                load_rows()
             if j < 4:
                 row_sums(2 * j - 4)
                 row_sums(2 * j - 3)
@@ -403,44 +449,35 @@ def tile_tromptcell_pb_kernel(
         regroup(b_, 0)
         turn_to_columns(b_, 1)
         regroup(b_, 1)
-        multiply(a)
         deviation(d)
+        rows_ps = rows_to_psum()
+        multiply(a)
+
         finish(a)
-        turn_to_features(c, 0)
-        affine(c, 0)
-        turn_to_features(c, 1)
-        affine(c, 1)
         quantise_mask(c)
-        quantise(b_)
+        quantise_mask(d)
         invert(d)
         negate(d)
-        quantise_mask(d)
-        normalise_first(d)
-        normalise(d, (1, 2, 3), on_vector=True)
-        turn_to_features(c, 2)
-        affine(c, 2)
-        turn_to_features(c, 3)
-        affine(c, 3)
+        norm_gpsimd(d, LAST)
+        quantise(b_)
+        norm_first_half(d, (0, 1, 2), rows_ps)
+        for b in range(FEATURE_BLOCKS):
+            turn_to_features(c, b)
+            affine(c, b)
 
-        turn_to_features(d, 0)
-        affine(d, 0, on_vector=True)
+
+        norm_second_half(d, (0, 1, 2), rows_ps)
         turn_to_columns(c, 0)
         regroup(c, 0)
-        turn_to_features(d, 1)
-        affine(d, 1)
         turn_to_columns(c, 1)
-        regroup(c, 1, on_vector=True)
-        turn_to_features(d, 2)
-        affine(d, 2, on_vector=True)
-        turn_to_features(d, 3)
-        affine(d, 3)
-        quantise(c)
-        turn_to_columns(d, 0)
-        regroup(d, 0)
-        turn_to_columns(d, 1)
-        regroup(d, 1, on_vector=True)
+        regroup(c, 1)
+        interleave(d, 0)
+
+        interleave(d, 1, on_scalar=True)
         multiply(b_)
         finish(b_)
+        quantise(c)
+
         quantise(d, 0, HALF)
         multiply(c, in_drain=True)
         finish(c)
@@ -448,4 +485,5 @@ def tile_tromptcell_pb_kernel(
         multiply(d, 0, HALF, in_drain=True)
         finish(d, 0, HALF)
         multiply(d, HALF, FEATURES, in_drain=True)
+
         finish(d, HALF, FEATURES, on_vector=True)

@@ -67,8 +67,9 @@ def tile_tromptcell_pb_kernel(
         b_sb = [const.tile([P, FEATURES], BF16, name="b_sb%d" % t) for t in range(PACK)]
         w_sb = [const.tile([P, FEATURES], BF16, name="w_sb%d" % t) for t in range(PACK)]
         for t in (2, LAST, 0, 1):
-            nc.sync.dma_start(out=b_sb[t][:], in_=b_view[:, t, :])
-            nc.sync.dma_start(out=w_sb[t][:], in_=w_view[:, t, :])
+            for part in (slice(0, HALF), slice(HALF, FEATURES)) if t == 2 else (slice(0, FEATURES),):
+                nc.sync.dma_start(out=b_sb[t][:, part], in_=b_view[:, t, part])
+                nc.sync.dma_start(out=w_sb[t][:, part], in_=w_view[:, t, part])
         mask_sb = const.tile([P, SAMPLES, COLUMNS], BF16, name="mask_sb")
         for g in range(SAMPLES // MASK_GROUP):
             group = slice(g * MASK_GROUP, (g + 1) * MASK_GROUP)
@@ -365,7 +366,9 @@ def tile_tromptcell_pb_kernel(
                 stage(n, *rest, **how)
 
         mask_groups = SAMPLES // MASK_GROUP
-        embed(0, (2, LAST, 0))
+        embed(0, (2,), 0, HALF)
+        embed(0, (2,), HALF, FEATURES)
+        embed(0, (LAST, 0))
         nc.vector.tensor_copy(out=x_sb[:], in_=x_ps[:, :, 0:SAMPLES].rearrange("p t n -> p n t"))
         embed(0, (1,))
         relu(0)
@@ -376,7 +379,7 @@ def tile_tromptcell_pb_kernel(
         embed(1, range(PACK))
         relu(1)
         measure(0)
-        embed(2, (0,), 0, 64)
+        embed(2, (0,), 0, 128)
         measure_end(0)
         relu_last(1)
         deviation(0)
@@ -385,7 +388,7 @@ def tile_tromptcell_pb_kernel(
         transpose_mask(3)
 
         for j in range(2, SAMPLES - 1):
-            embed(j, (0,), 64, FEATURES)
+            embed(j, (0,), 128, FEATURES)
             due(quantise, j - 4)
             invert(j - 2)
             negate(j - 2)
@@ -402,7 +405,7 @@ def tile_tromptcell_pb_kernel(
             due(finish, j - 4)
             relu_last(j)
             measure(j - 1)
-            embed(j + 1, (0,), 0, 64)
+            embed(j + 1, (0,), 0, 128)
             measure_end(j - 1)
             deviation(j - 1)
             if j == 4:
@@ -412,7 +415,7 @@ def tile_tromptcell_pb_kernel(
                 row_sums(2 * j - 3)
 
         z, a, b_, c, d = range(SAMPLES - 5, SAMPLES)
-        embed(d, (0,), 64, FEATURES)
+        embed(d, (0,), 128, FEATURES)
         quantise(z)
         invert(b_)
         negate(b_)

from contextlib import ExitStack

import concourse.mybir as mybir
from concourse.masks import make_identity

F32 = mybir.dt.float32
BF16 = mybir.dt.bfloat16
U32 = mybir.dt.uint32
U8 = mybir.dt.uint8
FP8X4 = mybir.dt.float8_e4m3fn_x4
ALU = mybir.AluOpType
ACT = mybir.ActivationFunctionType

SAMPLES = 16
COLUMNS = 512
PROMPTS = 128
FEATURES = 512
EPS = 1e-5

P = 128
PACK = 4
PAIRS = 2
FEATURE_BLOCKS = FEATURES // P
HALF = FEATURES // 2
MASK_GROUP = 4
LARGEST_F32 = 3.4028234663852886e38
LAST = PACK - 1

FLOPS = 2 * SAMPLES * PROMPTS * COLUMNS * FEATURES


def tile_tromptcell_pb_kernel(
    tc, x, mask, feature_emb_weight, feature_emb_bias, ln_emb_w, ln_emb_b, W_exp, b_exp, out
):
    nc = tc.nc
    with ExitStack() as ctx:
        const = ctx.enter_context(tc.tile_pool(name="const", bufs=1))
        work = ctx.enter_context(tc.tile_pool(name="work", bufs=2))
        small = ctx.enter_context(tc.tile_pool(name="small", bufs=3))
        psum_const = ctx.enter_context(tc.psum_pool(name="psum_const", bufs=1))
        psum = ctx.enter_context(tc.psum_pool(name="psum", bufs=1))
        ctx.enter_context(tc.manual_schedule())

        x_rows = const.tile([P, COLUMNS], BF16, name="x_rows")
        x_first = const.tile([P, PACK], BF16, name="x_first")
        nc.scalar.dma_start(out=x_first[:], in_=x[0].rearrange("(p t) -> p t", t=PACK))
        nc.scalar.dma_start(out=x_rows[0:SAMPLES, :], in_=x)
        nc.scalar.dma_start(out=x_rows[SAMPLES : 2 * SAMPLES, :], in_=x)
        rows = const.tile([P, P], BF16, name="rows")
        nc.vector.memset(rows[:], 0.0)
        nc.scalar.dma_start(out=rows[0:4, :], in_=ln_emb_w.rearrange("(b d) -> b d", d=P))
        nc.scalar.dma_start(out=rows[4:8, :], in_=ln_emb_b.rearrange("(b d) -> b d", d=P))
        nc.scalar.dma_start(out=rows[8:9, :], in_=W_exp.rearrange("(o q) -> o q", o=1))
        nc.scalar.dma_start(out=rows[9:10, :], in_=b_exp.rearrange("(o q) -> o q", o=1))
        warm = const.tile([P, 1], F32, name="warm")
        nc.gpsimd.memset(warm[:], 1.0)
        nc.scalar.activation(out=warm[:], in_=warm[:], func=ACT.Sqrt)
        nc.vector.memset(x_rows[32:64, :], 0.0)
        nc.vector.memset(x_rows[64:128, :], 0.0)
        minus = {}
        for first in (LAST - 1, LAST):
            minus[first] = const.tile([P, PACK], F32, name="minus%d" % first)
            nc.vector.memset(minus[first][:, 0:first], -1.0)
            nc.vector.memset(minus[first][:, first:PACK], -1.0 / FEATURES)
        b_view = feature_emb_bias.rearrange("(p t) d -> p t d", t=PACK)
        w_view = feature_emb_weight.rearrange("(p t) d -> p t d", t=PACK)
        b_sb = [const.tile([P, FEATURES], BF16, name="b_sb%d" % t) for t in range(PACK)]
        w_sb = [const.tile([P, FEATURES], BF16, name="w_sb%d" % t) for t in range(PACK)]
        for t in (2, LAST, 0, 1):
            for part in (slice(0, HALF), slice(HALF, FEATURES)) if t == 2 else (slice(0, FEATURES),):
                nc.sync.dma_start(out=b_sb[t][:, part], in_=b_view[:, t, part])
                nc.sync.dma_start(out=w_sb[t][:, part], in_=w_view[:, t, part])
        mask_sb = const.tile([P, SAMPLES, COLUMNS], BF16, name="mask_sb")
        for g in range(SAMPLES // MASK_GROUP):
            group = slice(g * MASK_GROUP, (g + 1) * MASK_GROUP)
            nc.sync.dma_start(out=mask_sb[:, group, :], in_=mask[group].rearrange("n q c -> q n c"))

        ident_bf = const.tile([P, P], BF16, name="ident_bf")
        make_identity(nc, ident_bf[:])
        ident_f32 = const.tile([P, P], F32, name="ident_f32")
        make_identity(nc, ident_f32[:])

        x_ps = psum.tile([P, PACK, P], BF16, name="x_ps", tag="e_w", bufs=2)
        for t in range(PACK):
            nc.tensor.transpose(x_ps[:, t, :], x_rows[:].rearrange("n (p t) -> n t p", t=PACK)[:, t, :], ident_bf[:])
        x_sb = const.tile([P, SAMPLES, PACK], BF16, name="x_sb")

        bias_ps = [psum_const.tile([P, 2, FEATURES], BF16, name="bias_ps%d" % h) for h in range(2)]
        for t in range(PACK):
            nc.tensor.matmul(
                out=bias_ps[t // 2][:, t % 2, :], lhsT=ident_bf[:], rhs=b_sb[t][:], start=True, stop=True
            )

        cols_ps = psum.tile([P, P], BF16, name="cols_ps", tag="acc")
        nc.tensor.transpose(cols_ps[:], rows[:], ident_bf[:])
        cols = const.tile([P, 16], F32, name="cols")
        ln_w_col = [cols[:, b : b + 1] for b in range(FEATURE_BLOCKS)]
        ln_b_col = [cols[:, FEATURE_BLOCKS + b : FEATURE_BLOCKS + b + 1] for b in range(FEATURE_BLOCKS)]
        b_exp_col = cols[:, 9:10]
        one_plus_w_exp = const.tile([P, 1], F32, name="one_plus_w_exp")

        mask_words = const.tile([P, SAMPLES, PROMPTS, PAIRS], F32, name="mask_words", align_bytes=64)
        mask_codes = const.tile([P, SAMPLES * PROMPTS], U32, name="mask_codes", align_bytes=64)
        mask_scales = const.tile([P, SAMPLES * PROMPTS], U8, name="mask_scales", align_bytes=64)
        out_bias = const.tile([P, SAMPLES], F32, name="out_bias")
        ones = const.tile([P, 16], BF16, name="ones")
        nc.vector.memset(ones[:], 1.0)
        sums = psum.tile([P, SAMPLES], F32, name="sums", tag="acc")

        def first_scalar(n):
            return LAST - 1 if n in (0, 2) else LAST

        row_w = const.tile([P, FEATURES], BF16, name="row_w")
        row_b = const.tile([P, FEATURES], BF16, name="row_b")
        flat = const.tile([P, PACK, FEATURES], BF16, name="flat")

        act, stats, moments, std, neg_mean, e_t, grouped, total, spread = {}, {}, {}, {}, {}, {}, {}, {}, {}
        rstd, z_t, e_w, codes, scales, acc = {}, {}, {}, {}, {}, {}

        def embed(n, groups, first=0, last=FEATURES):
            if n not in act:
                act[n] = work.tile([P, PACK, FEATURES], F32, name="act", bufs=5)
            for t in groups:
                nc.vector.scalar_tensor_tensor(
                    out=act[n][:, t, first:last],
                    in0=w_sb[t][:, first:last],
                    scalar=x_first[:, t : t + 1] if n == 0 else x_sb[:, n, t : t + 1],
                    in1=b_sb[t][:, first:last] if n == 0 else bias_ps[t // 2][:, t % 2, first:last],
                    op0=ALU.mult,
                    op1=ALU.add,
                )

        def relu(n):
            mine = act[n][:, 0 : first_scalar(n), :]
            nc.gpsimd.tensor_scalar(out=mine, in0=mine, scalar1=LARGEST_F32, scalar2=0.0, op0=ALU.min, op1=ALU.max)

        def relu_last(n):
            moments[n] = small.tile([P, PACK, 2], F32, name="moments", bufs=4)
            for t in range(first_scalar(n), PACK):
                nc.scalar.activation(
                    out=act[n][:, t, :], in_=act[n][:, t, :], func=ACT.Relu, accum_out=moments[n][:, t, 0:1]
                )

        def square_last(n):
            for t in range(first_scalar(n), PACK):
                squares = work.tile([P, FEATURES], BF16, name="squares")
                nc.scalar.activation(
                    out=squares[:], in_=act[n][:, t, :], func=ACT.Square,
                    scale=-float(FEATURES), bias=moments[n][:, t, 0:1], accum_out=moments[n][:, t, 1:2],
                )

        def measure(n):
            stats[n] = small.tile([P, LAST, 6], F32, name="stats")
            for t in range(first_scalar(n)):
                nc.vector.bn_stats(out=stats[n][:, t, :], in_=act[n][:, t, :])
            for t in range(first_scalar(n) - 1):
                nc.vector.bn_aggr(out=moments[n][:, t, :], in_=stats[n][:, t, :])

        def measure_end(n):
            t = first_scalar(n) - 1
            nc.vector.bn_aggr(out=moments[n][:, t, :], in_=stats[n][:, t, :])

        def deviation(n):
            std[n] = small.tile([P, PACK], F32, name="std")
            first = first_scalar(n)
            nc.scalar.activation(out=std[n][:, 0:first], in_=moments[n][:, 0:first, 1], func=ACT.Sqrt, bias=EPS)
            nc.scalar.activation(
                out=std[n][:, first:PACK], in_=moments[n][:, first:PACK, 1], func=ACT.Sqrt,
                scale=1.0 / FEATURES**3, bias=EPS,
            )

        def negate(n):
            neg_mean[n] = small.tile([P, PACK], F32, name="neg_mean")
            nc.vector.tensor_tensor(
                out=neg_mean[n][:], in0=moments[n][:, :, 0], in1=minus[first_scalar(n)][:], op=ALU.mult
            )

        def invert(n):
            rstd[n] = small.tile([P, PACK], F32, name="rstd")
            nc.vector.reciprocal(out=rstd[n][:], in_=std[n][:])

        def load_rows():
            for vector, tile in ((ln_emb_w, row_w), (ln_emb_b, row_b)):
                nc.sync.dma_start(out=tile[:], in_=vector.partition_broadcast(P))

        def rows_to_psum():
            rows_ps = psum_const.tile([P, 2, FEATURES], BF16, name="bias_ps0")
            for k, tile in ((0, row_w), (1, row_b)):
                nc.tensor.matmul(out=rows_ps[:, k, :], lhsT=ident_bf[:], rhs=tile[:], start=True, stop=True)
            return rows_ps

        def norm_first_half(n, groups, rows_ps):
            for t in groups:
                nc.vector.scalar_tensor_tensor(
                    out=act[n][:, t, :], in0=act[n][:, t, :], scalar=neg_mean[n][:, t : t + 1],
                    in1=rows_ps[:, 0, :], op0=ALU.add, op1=ALU.mult,
                )

        def norm_second_half(n, groups, rows_ps):
            for t in groups:
                nc.vector.scalar_tensor_tensor(
                    out=flat[:, t, :], in0=act[n][:, t, :], scalar=rstd[n][:, t : t + 1],
                    in1=rows_ps[:, 1, :], op0=ALU.mult, op1=ALU.add,
                )

        def norm_gpsimd(n, t):
            normalise(n, (t,))
            nc.gpsimd.tensor_tensor(out=act[n][:, t, :], in0=act[n][:, t, :], in1=row_w[:], op=ALU.mult)
            nc.gpsimd.tensor_tensor(out=flat[:, t, :], in0=act[n][:, t, :], in1=row_b[:], op=ALU.add)

        def interleave(n, h, on_scalar=False):
            if h == 0:
                grouped[n] = work.tile([P, FEATURES, PAIRS], F32, name="grouped", align_bytes=64)
            mine = slice(h * HALF, (h + 1) * HALF)
            target = grouped[n][:].rearrange("p d u -> p (d u)").bitcast(BF16).rearrange("p (d t) -> p d t", t=PACK)[:, mine, :]
            source = flat[:].rearrange("p t d -> p d t")[:, mine, :]
            if on_scalar:
                nc.scalar.copy(out=target, in_=source)
            else:
                nc.vector.tensor_copy(out=target, in_=source)

        def normalise_first(n):
            nc.vector.tensor_scalar(
                out=act[n][:, 0, :], in0=act[n][:, 0, :], scalar1=moments[n][:, 0, 0:1], scalar2=rstd[n][:, 0:1],
                op0=ALU.subtract, op1=ALU.mult,
            )

        def normalise(n, groups, on_vector=False):
            engine = nc.vector if on_vector else nc.gpsimd
            for t in groups:
                engine.tensor_scalar(
                    out=act[n][:, t, :], in0=act[n][:, t, :], scalar1=neg_mean[n][:, t : t + 1],
                    scalar2=rstd[n][:, t : t + 1], op0=ALU.add, op1=ALU.mult,
                )

        def turn_to_features(n, b):
            z_t[n, b] = psum.tile([P, PACK, P], F32, name="z_t", tag="z_t", bufs=3)
            for t in range(PACK):
                nc.tensor.transpose(z_t[n, b][:, t, :], act[n][:, t, b * P : (b + 1) * P], ident_f32[:])

        def affine(n, b, on_vector=False):
            if b == 0:
                e_t[n] = work.tile([P, FEATURE_BLOCKS, COLUMNS], BF16, name="e_t")
            target = e_t[n][:, b, :].rearrange("d (u p e) -> d u p e", u=PAIRS, e=2)
            source = z_t[n, b][:].rearrange("d (u e) p -> d u p e", e=2)
            if on_vector:
                nc.vector.tensor_scalar(
                    out=target, in0=source, scalar1=ln_w_col[b], scalar2=ln_b_col[b], op0=ALU.mult, op1=ALU.add
                )
            else:
                nc.scalar.activation(out=target, in_=source, func=ACT.Identity, scale=ln_w_col[b], bias=ln_b_col[b])

        def turn_to_columns(n, h):
            e_w[n, h] = psum.tile([P, PAIRS, HALF], F32, name="e_w", tag="e_w", bufs=2)
            for i in range(HALF // P):
                words = e_t[n][:, h * (HALF // P) + i, :].bitcast(F32)
                for u in range(PAIRS):
                    nc.tensor.transpose(
                        e_w[n, h][:, u, i * P : (i + 1) * P], words[:, u * P : (u + 1) * P], ident_f32[:]
                    )

        def regroup(n, h, on_vector=False):
            if h == 0:
                grouped[n] = work.tile([P, FEATURES, PAIRS], F32, name="grouped", align_bytes=64)
            target = grouped[n][:, h * HALF : (h + 1) * HALF, :]
            source = e_w[n, h][:].rearrange("p u d -> p d u")
            if on_vector:
                nc.vector.tensor_copy(out=target, in_=source)
            else:
                nc.scalar.copy(out=target, in_=source)

        def quantise(n, first=0, last=FEATURES):
            if first == 0:
                codes[n] = work.tile([P, FEATURES], U32, name="codes", bufs=4, align_bytes=64)
                scales[n] = work.tile([P, FEATURES], U8, name="scales", bufs=4, align_bytes=64)
            nc.vector.quantize_mx(
                out=codes[n][:, first:last].bitcast(FP8X4),
                scales=scales[n][:, first:last],
                in_=grouped[n][:, first:last, :].rearrange("p d u -> p (d u)").bitcast(BF16),
            )

        def multiply(n, first=0, last=FEATURES, in_drain=False):
            prompts = slice(n * PROMPTS, (n + 1) * PROMPTS)
            if in_drain:
                acc[n] = psum.tile([P, FEATURES], F32, name="acc_end", tag="z_t", bufs=3)
            else:
                acc[n] = psum.tile([P, FEATURES], F32, name="acc", tag="acc")
            nc.tensor.matmul_mx(
                out=acc[n][:, first:last],
                lhsT=mask_codes[:, prompts].bitcast(FP8X4),
                lhsT_scale=mask_scales[:, prompts],
                rhs=codes[n][:, first:last].bitcast(FP8X4),
                rhs_scale=scales[n][:, first:last],
                start=True,
                stop=True,
            )

        def finish(n, first=0, last=FEATURES, on_vector=False):
            result = work.tile([P, FEATURES], F32, name="result", bufs=6)
            scale, bias = one_plus_w_exp[:, 0:1], out_bias[:, n : n + 1]
            if on_vector:
                nc.vector.tensor_scalar(
                    out=result[:, first:last], in0=acc[n][:, first:last], scalar1=scale, scalar2=bias,
                    op0=ALU.mult, op1=ALU.add,
                )
            else:
                nc.scalar.activation(
                    out=result[:, first:last], in_=acc[n][:, first:last], func=ACT.Identity, scale=scale, bias=bias
                )
            nc.sync.dma_start(out=out[n, :, first:last], in_=result[:, first:last])

        def to_features(n):
            for b in range(FEATURE_BLOCKS):
                turn_to_features(n, b)
                affine(n, b)

        def to_columns(n):
            for h in range(FEATURES // HALF):
                turn_to_columns(n, h)
                regroup(n, h)

        def pool(n):
            quantise(n)
            multiply(n)
            finish(n)

        def take_vectors():
            nc.scalar.copy(out=cols[:], in_=cols_ps[:, 0:16])
            nc.gpsimd.tensor_scalar_add(out=one_plus_w_exp[:], in0=cols[:, 8:9], scalar1=1.0)

        def row_sums(g):
            for n in range(g * MASK_GROUP, (g + 1) * MASK_GROUP):
                values = (
                    mask_words[:, n, :, :].rearrange("p q u -> p (q u)").bitcast(BF16)
                    .rearrange("p (q t) -> p t q", t=PACK)
                )
                for t in range(PACK):
                    nc.tensor.matmul(
                        out=sums[:, n : n + 1], lhsT=values[:, t, :], rhs=ones[:, 0:1],
                        start=(t == 0), stop=(t == PACK - 1),
                    )
            if g == SAMPLES // MASK_GROUP - 1:
                nc.scalar.activation(out=out_bias[:], in_=sums[:], func=ACT.Copy, scale=b_exp_col)

        def transpose_mask(g):
            for first in range(g * MASK_GROUP, (g + 1) * MASK_GROUP, 2):
                m_t = psum.tile([P, 2, PAIRS, PROMPTS], F32, name="m_t", tag="z_t", bufs=3)
                for s in range(2):
                    words = mask_sb[:, first + s, :].bitcast(F32).rearrange("q (p u) -> q u p", u=PAIRS)
                    for u in range(PAIRS):
                        nc.tensor.transpose(m_t[:, s, u, :], words[:, u, :], ident_f32[:])
                nc.scalar.copy(
                    out=mask_words[:, first : first + 2, :, :], in_=m_t[:].rearrange("p s u q -> p s q u")
                )

        def quantise_mask(n):
            prompts = slice(n * PROMPTS, (n + 1) * PROMPTS)
            nc.vector.quantize_mx(
                out=mask_codes[:, prompts].bitcast(FP8X4),
                scales=mask_scales[:, prompts],
                in_=mask_words[:, n, :, :].rearrange("p q u -> p (q u)").bitcast(BF16),
            )

        def due(stage, n, *rest, **how):
            if 0 <= n < SAMPLES:
                stage(n, *rest, **how)

        mask_groups = SAMPLES // MASK_GROUP
        embed(0, (2,), 0, HALF)
        embed(0, (2,), HALF, FEATURES)
        embed(0, (LAST, 0))
        nc.vector.tensor_copy(out=x_sb[:], in_=x_ps[:, :, 0:SAMPLES].rearrange("p t n -> p n t"))
        embed(0, (1,))
        relu(0)
        relu_last(0)
        square_last(0)
        transpose_mask(0)
        transpose_mask(1)
        embed(1, range(PACK))
        relu(1)
        measure(0)
        embed(2, (0,), 0, 128)
        measure_end(0)
        relu_last(1)
        deviation(0)
        take_vectors()
        transpose_mask(2)
        transpose_mask(3)

        for j in range(2, SAMPLES - 1):
            embed(j, (0,), 128, FEATURES)
            due(quantise, j - 4)
            invert(j - 2)
            negate(j - 2)
            due(quantise_mask, j - 3)
            if j > 2:
                normalise_first(j - 2)
            embed(j, (1, 2, 3))
            normalise(j - 2, range(0 if j == 2 else 1, PACK))
            relu(j)
            due(to_features, j - 3)
            square_last(j - 1)
            due(to_columns, j - 3)
            due(multiply, j - 4)
            due(finish, j - 4)
            relu_last(j)
            measure(j - 1)
            embed(j + 1, (0,), 0, 128)
            measure_end(j - 1)
            deviation(j - 1)
            if j == 4:
                load_rows()
            if j < 4:
                row_sums(2 * j - 4)
                row_sums(2 * j - 3)

        z, a, b_, c, d = range(SAMPLES - 5, SAMPLES)
        embed(d, (0,), 128, FEATURES)
        quantise(z)
        invert(b_)
        negate(b_)
        quantise_mask(a)
        normalise_first(b_)
        embed(d, (1, 2, 3))
        normalise(b_, (1, 2, 3))
        relu(d)
        to_features(a)
        square_last(c)
        to_columns(a)
        multiply(z)
        relu_last(d)
        finish(z)
        measure(c)
        measure_end(c)
        deviation(c)

        turn_to_features(b_, 0)
        affine(b_, 0, on_vector=True)
        quantise(a)
        invert(c)
        negate(c)
        quantise_mask(b_)
        normalise_first(c)
        normalise(c, (1, 2, 3))
        for b in (1, 2, 3):
            turn_to_features(b_, b)
            affine(b_, b)
        square_last(d)
        measure(d)
        measure_end(d)
        turn_to_columns(b_, 0)
        regroup(b_, 0)
        turn_to_columns(b_, 1)
        regroup(b_, 1)
        deviation(d)
        rows_ps = rows_to_psum()
        multiply(a)

        finish(a)
        quantise_mask(c)
        quantise_mask(d)
        invert(d)
        negate(d)
        norm_gpsimd(d, LAST)
        quantise(b_)
        norm_first_half(d, (0, 1, 2), rows_ps)
        for b in range(FEATURE_BLOCKS):
            turn_to_features(c, b)
            affine(c, b)


        norm_second_half(d, (0, 1, 2), rows_ps)
        turn_to_columns(c, 0)
        regroup(c, 0)
        turn_to_columns(c, 1)
        regroup(c, 1)
        interleave(d, 0)

        interleave(d, 1, on_scalar=True)
        multiply(b_)
        finish(b_)
        quantise(c)

        quantise(d, 0, HALF)
        multiply(c, in_drain=True)
        finish(c)
        quantise(d, HALF, FEATURES)
        multiply(d, 0, HALF, in_drain=True)
        finish(d, 0, HALF)
        multiply(d, HALF, FEATURES, in_drain=True)

        finish(d, HALF, FEATURES, on_vector=True)
